import numpy as np
import ml_dtypes


def mxq(x, axis, fmt="e4m3"):
    dtype, down = {"e4m3": (ml_dtypes.float8_e4m3fn, 7), "e5m2": (ml_dtypes.float8_e5m2, 14)}[fmt]
    v = np.moveaxis(np.asarray(x, np.float32).astype(ml_dtypes.bfloat16).astype(np.float64), axis, -1)
    blocks = v.reshape(v.shape[:-1] + (-1, 32))
    amax = np.abs(blocks).max(-1, keepdims=True)
    byte = np.maximum(np.where(amax > 0, np.frexp(amax)[1] - 1 + 127, 0) - down, 1)
    scale = np.exp2(byte - 127.0)
    codes = (blocks / scale).astype(np.float32).astype(dtype).astype(np.float64)
    return np.moveaxis((codes * scale).reshape(v.shape), -1, axis)


WIDE = False


def mx_kscale(k):
    if not WIDE:
        return np.ones(k)
    levels = np.array([10, -10, 5, -5, 0])
    a = np.random.permutation(np.resize(levels, k // 512 * 4)).reshape(k // 512, 4)
    idx = np.arange(k)
    return np.exp2(a[idx // 512, idx % 128 // 32])


BF16 = ml_dtypes.bfloat16


def bf(x):
    return np.asarray(x, np.float32).astype(BF16)


def f64(x):
    return np.asarray(x).astype(np.float64)


E2M1 = np.array([0.0, 0.5, 1.0, 1.5, 2.0, 3.0, 4.0, 6.0, -0.0, -0.5, -1.0, -1.5, -2.0, -3.0, -4.0, -6.0])


def pack_weight(w, fmt):
    k, n = w.shape
    w = f64(bf(w)).reshape(k // 32, 32, n)
    amax = np.abs(w).max(1)
    if fmt == "e4m3":
        byte = np.frexp(amax)[1] - 1 + 127 - 7
    else:
        mant, ex = np.frexp(amax / 6.0)
        byte = np.where(mant > 0.5, ex, ex - 1) + 127
    byte = np.clip(np.where(amax > 0, byte, 1), 1, 254)
    scaled = (w * np.exp2(127.0 - byte)[:, None, :]).reshape(k, n).astype(np.float32)
    by_word = np.ascontiguousarray(scaled.reshape(k // 512, 128, 4, n).transpose(0, 1, 3, 2))
    if fmt == "e4m3":
        words = by_word.astype(ml_dtypes.float8_e4m3fn).view(np.uint8)
    else:
        c = by_word.astype(ml_dtypes.float4_e2m1fn).view(np.uint8) & 0xF
        words = c[..., 0::2] | (c[..., 1::2] << 4)
    return np.ascontiguousarray(words), np.ascontiguousarray(byte.astype(np.uint8).reshape(k // 512, 16, n))


def unpack_weight(words, scales, fmt):
    g, p, n, _ = words.shape
    if fmt == "e4m3":
        vals = np.ascontiguousarray(words).view(ml_dtypes.float8_e4m3fn).astype(np.float64)
    else:
        nib = np.empty((g, p, n, 4), np.uint8)
        nib[..., 0::2] = words & 0xF
        nib[..., 1::2] = words >> 4
        vals = E2M1[nib]
    vals = vals * np.repeat(np.exp2(scales.astype(np.float64) - 127.0), 8, axis=1)[..., None]
    return vals.transpose(0, 1, 3, 2).reshape(g * 512, n)

def pack4(w):
    words, scales = pack_weight(w, "e2m1")
    return words.reshape(words.shape[0], 128, -1), scales


def unpack4(words, scales):
    return unpack_weight(words.reshape(words.shape[0], 128, -1, 2), scales, "e2m1")


B, N, D = 4, 32, 4096
C = 2 * D
EPS_BN = 1e-5
NEG_SLOPE = 0.01


def bn_lrelu(x, g, b):
    mean = np.mean(x, axis=(0, 2), keepdims=True)
    var = np.var(x, axis=(0, 2), keepdims=True)
    y = (x - mean) / np.sqrt(var + EPS_BN) * g[None, :, None] + b[None, :, None]
    return np.where(y >= 0, y, NEG_SLOPE * y)


def setup_inputs():
    s = mx_kscale(C)
    v = np.random.standard_normal((B, C, N))
    w2 = np.random.standard_normal((D, C)) / np.sqrt(C) / s[None, :]
    words, scales = pack4(np.ascontiguousarray(w2.T))
    return {"h1": bf(np.where(v >= 0, v, NEG_SLOPE * v) * s[None, :, None]),
            "W2_words": words,
            "W2_scales": scales,
            "g2": bf(1.0 + 0.2 * np.random.standard_normal(D)),
            "b2": bf(0.3 * np.random.standard_normal(D))}


def reference(h1, W2_words, W2_scales, g2, b2):
    z = unpack4(W2_words, W2_scales).T @ mxq(f64(h1), 1, "e4m3")
    return np.swapaxes(bn_lrelu(z, f64(g2), f64(b2)), 1, 2)

@@ -1,0 +1,219 @@
+import concourse.mybir as mybir
+from concourse.masks import make_identity
+
+F32 = mybir.dt.float32
+BF16 = mybir.dt.bfloat16
+I32 = mybir.dt.int32
+U32 = mybir.dt.uint32
+U8 = mybir.dt.uint8
+FP8X4 = mybir.dt.float8_e4m3fn_x4
+FP4X4 = mybir.dt.float4_e2m1fn_x4
+ALU = mybir.AluOpType
+ACT = mybir.ActivationFunctionType
+
+P = 128
+PACK = 4
+K_PASS = P * PACK
+GRAPHS, NODES = 4, 32
+C_IN = 8192
+C_OUT = 4096
+PASSES = C_IN // K_PASS
+BANK = 512
+CHUNK = 1024
+BANKS = CHUNK // BANK
+CHUNKS = C_OUT // CHUNK
+BLOCKS = BANK // P
+TILES = CHUNK // P
+PIECE = 4
+PIECES = PASSES // PIECE
+AHEAD = 8
+SCALE_RUN = 8
+EPS_BN = 1e-5
+NEG_SLOPE = 0.01
+
+FLOPS = 2 * GRAPHS * NODES * C_OUT * C_IN
+
+
+def tile_yuyipointupdate_pb_k_kernel(tc, h1, w_words, w_scales, g2, b2, out):
+    nc = tc.nc
+    words_i32 = w_words.bitcast(I32)
+    scales_i32 = w_scales.bitcast(I32)
+    out_rows = out.rearrange("b n o -> (b n) o")
+
+    with tc.manual_schedule(), tc.tile_pool(name="keep", bufs=1) as keep, tc.tile_pool(
+        name="raw", bufs=GRAPHS
+    ) as raw_pool, tc.tile_pool(name="weights", bufs=AHEAD + 1) as w_pool, tc.tile_pool(
+        name="work", bufs=2 * BANKS
+    ) as work, tc.tile_pool(name="small", bufs=2) as small, tc.psum_pool(
+        name="psum_z", bufs=2 * BANKS
+    ) as psum_z, tc.psum_pool(name="psum_zt", bufs=BANKS) as psum_zt, tc.psum_pool(
+        name="psum_rt", bufs=BANKS
+    ) as psum_rt:
+        gain_shift_rows = keep.tile([P, P], BF16)
+        nc.vector.memset(gain_shift_rows[:], 0.0)
+        eps = keep.tile([P, 1], F32)
+        nc.vector.memset(eps[:], EPS_BN)
+        rows = C_OUT // P
+        nc.scalar.dma_start(out=gain_shift_rows[0:rows, :], in_=g2.rearrange("(m p) -> m p", p=P))
+        nc.scalar.dma_start(out=gain_shift_rows[rows : 2 * rows, :], in_=b2.rearrange("(m p) -> m p", p=P))
+        ident = keep.tile([P, P], F32)
+        make_identity(nc, ident[:])
+
+        planes = []
+        for c in range(CHUNKS):
+            plane = keep.tile([P, PASSES, CHUNK], U8, name="plane%d" % c, align_bytes=64)
+            nc.vector.memset(plane[:].bitcast(I32), 0)
+            planes.append(plane)
+
+        raws = []
+        for b in range(GRAPHS):
+            raw = raw_pool.tile([P, PASSES, PACK, NODES], BF16, name="raw")
+            nc.sync.dma_start(
+                out=raw[:].rearrange("p g t n -> p g (t n)"),
+                in_=h1[b].rearrange("(g p t) n -> p g (t n)", g=PASSES, p=P, t=PACK),
+            )
+            raws.append(raw)
+
+        def load_scales(c):
+            cols = slice(c * CHUNK // 4, (c + 1) * CHUNK // 4)
+            for g0 in range(0, PASSES, SCALE_RUN):
+                for q in range(8):
+                    first = 32 * (q // 4) + q % 4
+                    nc.sync.dma_start(
+                        out=planes[c][first:P:64, g0 : g0 + SCALE_RUN, :].bitcast(I32),
+                        in_=scales_i32[g0 : g0 + SCALE_RUN, q:16:8, cols].rearrange("g q n -> q g n"),
+                    )
+
+        w_tiles = {}
+
+        def load_piece(i):
+            c, piece = divmod(i, PIECES)
+            if piece == 0:
+                load_scales(c)
+            w_tile = w_pool.tile([P, PIECE, 2 * CHUNK], U8, name="w_tile", align_bytes=64)
+            nc.sync.dma_start(
+                out=w_tile[:].bitcast(I32),
+                in_=words_i32[
+                    piece * PIECE : (piece + 1) * PIECE, :, c * CHUNK // 2 : (c + 1) * CHUNK // 2
+                ].rearrange("g p n -> p g n"),
+            )
+            w_tiles[i] = w_tile
+
+        for i in range(AHEAD):
+            load_piece(i)
+
+        gain_shift_f32 = keep.tile([P, P], F32)
+        nc.vector.tensor_copy(out=gain_shift_f32[:], in_=gain_shift_rows[:])
+        gs_ps = psum_zt.tile([P, BLOCKS, P], F32, name="zt")
+        nc.tensor.transpose(gs_ps[:, 0, :], gain_shift_f32[:], ident[:])
+        gain_shift = keep.tile([P, 2 * rows], F32)
+        nc.vector.tensor_copy(out=gain_shift[:], in_=gs_ps[:, 0, 0 : 2 * rows])
+
+        grouped = keep.tile([P, PASSES, P, PACK], BF16, align_bytes=64)
+        for b in range(GRAPHS):
+            nc.vector.tensor_copy(
+                out=grouped[:, :, b * NODES : (b + 1) * NODES, :],
+                in_=raws[b][:].rearrange("p g t n -> p g n t"),
+            )
+        h_codes = keep.tile([P, PASSES, P], U32, align_bytes=64)
+        h_scales = keep.tile([P, PASSES, P], U8, align_bytes=64)
+        half = PASSES // 2
+        for g0 in range(0, PASSES, half):
+            nc.vector.quantize_mx(
+                out=h_codes[:, g0 : g0 + half, :].rearrange("p g c -> p (g c)").bitcast(FP8X4),
+                scales=h_scales[:, g0 : g0 + half, :].rearrange("p g c -> p (g c)"),
+                in_=grouped[:, g0 : g0 + half, :, :].rearrange("p g c t -> p (g c t)"),
+            )
+
+        def normalise(c, z_banks):
+            zt_banks = []
+            for u in range(BANKS):
+                z_sb = work.tile([P, BANK], F32, name="z_sb")
+                if u % 2 == 0:
+                    nc.scalar.copy(out=z_sb[:], in_=z_banks[u][:])
+                else:
+                    nc.vector.tensor_copy(out=z_sb[:], in_=z_banks[u][:])
+                zt = psum_zt.tile([P, BLOCKS, P], F32, name="zt")
+                for j in range(BLOCKS):
+                    nc.tensor.transpose(zt[:, j, :], z_sb[:, j * P : (j + 1) * P], ident[:])
+                zt_banks.append(zt)
+
+            stats = small.tile([P, TILES, 6], F32, name="stats")
+            mean_var = small.tile([P, TILES, 2], F32, name="mean_var")
+            for m in range(TILES):
+                nc.vector.bn_stats(out=stats[:, m, :], in_=zt_banks[m // BLOCKS][:, m % BLOCKS, :])
+            for m in range(TILES):
+                nc.vector.bn_aggr(out=mean_var[:, m, :], in_=stats[:, m, :])
+            std = small.tile([P, TILES], F32, name="std")
+            nc.scalar.activation(out=std[:], in_=mean_var[:, :, 1], func=ACT.Sqrt, bias=eps[:, 0:1], scale=1.0)
+            rstd = small.tile([P, TILES], F32, name="rstd")
+            nc.vector.reciprocal(out=rstd[:], in_=std[:])
+            scale = small.tile([P, TILES], F32, name="scale")
+            nc.vector.tensor_tensor(
+                out=scale[:], in0=rstd[:], in1=gain_shift[:, c * TILES : (c + 1) * TILES], op=ALU.mult
+            )
+            mean_scaled = small.tile([P, TILES], F32, name="mean_scaled")
+            nc.vector.tensor_tensor(out=mean_scaled[:], in0=mean_var[:, :, 0], in1=scale[:], op=ALU.mult)
+            bias = small.tile([P, TILES], F32, name="bias")
+            nc.vector.tensor_tensor(
+                out=bias[:],
+                in0=gain_shift[:, rows + c * TILES : rows + (c + 1) * TILES],
+                in1=mean_scaled[:],
+                op=ALU.subtract,
+            )
+            results = []
+            for u in range(BANKS):
+                y = work.tile([P, BLOCKS, P], F32, name="y")
+                for j in range(BLOCKS):
+                    m = u * BLOCKS + j
+                    nc.scalar.activation(
+                        out=y[:, j, :],
+                        in_=zt_banks[u][:, j, :],
+                        func=ACT.Identity,
+                        bias=bias[:, m : m + 1],
+                        scale=scale[:, m : m + 1],
+                    )
+                r = work.tile([P, BLOCKS, P], F32, name="r")
+                nc.vector.scalar_tensor_tensor(
+                    out=r[:], in0=y[:], scalar=NEG_SLOPE, in1=y[:], op0=ALU.mult, op1=ALU.max
+                )
+                results.append(r)
+            return results
+
+        def finish(c, results):
+            for u in range(BANKS):
+                rt = psum_rt.tile([P, BANK], F32, name="rt")
+                for j in range(BLOCKS):
+                    nc.tensor.transpose(rt[:, j * P : (j + 1) * P], results[u][:, j, :], ident[:])
+                o_sb = work.tile([P, BANK], F32, name="o_sb")
+                if u % 2 == 0:
+                    nc.scalar.copy(out=o_sb[:], in_=rt[:])
+                else:
+                    nc.vector.tensor_copy(out=o_sb[:], in_=rt[:])
+                o0 = c * CHUNK + u * BANK
+                nc.scalar.dma_start(out=out_rows[:, o0 : o0 + BANK], in_=o_sb[:])
+
+        results = None
+        for c in range(CHUNKS):
+            z_banks = [psum_z.tile([P, BANK], F32, name="z") for u in range(BANKS)]
+            for piece in range(PIECES):
+                i = c * PIECES + piece
+                if i + AHEAD < CHUNKS * PIECES:
+                    load_piece(i + AHEAD)
+                w_tile = w_tiles[i]
+                for k in range(PIECE):
+                    g = piece * PIECE + k
+                    for u in range(BANKS):
+                        nc.tensor.matmul_mx(
+                            out=z_banks[u][:],
+                            lhsT=h_codes[:, g, :].bitcast(FP8X4),
+                            lhsT_scale=h_scales[:, g, :],
+                            rhs=w_tile[:, k, 2 * u * BANK : 2 * (u + 1) * BANK].bitcast(FP4X4),
+                            rhs_scale=planes[c][:, g, u * BANK : (u + 1) * BANK],
+                            start=(g == 0),
+                            stop=(g == PASSES - 1),
+                        )
+                if piece == 0 and c > 0:
+                    finish(c - 1, results)
+            results = normalise(c, z_banks)
+        finish(CHUNKS - 1, results)

@@ -19,12 +19,9 @@ C_IN = 8192
 C_OUT = 4096
 PASSES = C_IN // K_PASS
 BANK = 512
-CHUNK = 1024
-BANKS = CHUNK // BANK
-CHUNKS = C_OUT // CHUNK
 BLOCKS = BANK // P
-TILES = CHUNK // P
-PIECE = 4
+CHUNK_BANKS = (4, 2, 2)
+PIECE = 2
 PIECES = PASSES // PIECE
 AHEAD = 8
 SCALE_RUN = 8
@@ -39,16 +36,18 @@ def tile_yuyipointupdate_pb_k_kernel(tc, h1, w_words, w_scales, g2, b2, out):
     words_i32 = w_words.bitcast(I32)
     scales_i32 = w_scales.bitcast(I32)
     out_rows = out.rearrange("b n o -> (b n) o")
+    first_bank = [sum(CHUNK_BANKS[:c]) for c in range(len(CHUNK_BANKS))]
+    widest = max(CHUNK_BANKS) * BANK
 
     with tc.manual_schedule(), tc.tile_pool(name="keep", bufs=1) as keep, tc.tile_pool(
         name="raw", bufs=GRAPHS
     ) as raw_pool, tc.tile_pool(name="weights", bufs=AHEAD + 1) as w_pool, tc.tile_pool(
-        name="work", bufs=2 * BANKS
-    ) as work, tc.tile_pool(name="small", bufs=2) as small, tc.psum_pool(
-        name="psum_z", bufs=2 * BANKS
-    ) as psum_z, tc.psum_pool(name="psum_zt", bufs=BANKS) as psum_zt, tc.psum_pool(
-        name="psum_rt", bufs=BANKS
-    ) as psum_rt:
+        name="work", bufs=3
+    ) as work, tc.tile_pool(name="results", bufs=max(CHUNK_BANKS) + 2) as res_pool, tc.tile_pool(
+        name="small", bufs=3
+    ) as small, tc.psum_pool(name="psum_z", bufs=max(CHUNK_BANKS)) as psum_z, tc.psum_pool(
+        name="psum_zt", bufs=2
+    ) as psum_zt, tc.psum_pool(name="psum_rt", bufs=2) as psum_rt:
         gain_shift_rows = keep.tile([P, P], BF16)
         nc.vector.memset(gain_shift_rows[:], 0.0)
         eps = keep.tile([P, 1], F32)
@@ -60,8 +59,8 @@ def tile_yuyipointupdate_pb_k_kernel(tc, h1, w_words, w_scales, g2, b2, out):
         make_identity(nc, ident[:])
 
         planes = []
-        for c in range(CHUNKS):
-            plane = keep.tile([P, PASSES, CHUNK], U8, name="plane%d" % c, align_bytes=64)
+        for c in range(len(CHUNK_BANKS)):
+            plane = keep.tile([P, PASSES, CHUNK_BANKS[c] * BANK], U8, name="plane%d" % c, align_bytes=64)
             nc.vector.memset(plane[:].bitcast(I32), 0)
             planes.append(plane)
 
@@ -75,7 +74,8 @@ def tile_yuyipointupdate_pb_k_kernel(tc, h1, w_words, w_scales, g2, b2, out):
             raws.append(raw)
 
         def load_scales(c):
-            cols = slice(c * CHUNK // 4, (c + 1) * CHUNK // 4)
+            o0 = first_bank[c] * BANK
+            cols = slice(o0 // 4, (o0 + CHUNK_BANKS[c] * BANK) // 4)
             for g0 in range(0, PASSES, SCALE_RUN):
                 for q in range(8):
                     first = 32 * (q // 4) + q % 4
@@ -90,11 +90,13 @@ def tile_yuyipointupdate_pb_k_kernel(tc, h1, w_words, w_scales, g2, b2, out):
             c, piece = divmod(i, PIECES)
             if piece == 0:
                 load_scales(c)
-            w_tile = w_pool.tile([P, PIECE, 2 * CHUNK], U8, name="w_tile", align_bytes=64)
+            o0 = first_bank[c] * BANK
+            width = CHUNK_BANKS[c] * BANK
+            w_tile = w_pool.tile([P, PIECE, 2 * widest], U8, name="w_tile", align_bytes=64)
             nc.sync.dma_start(
-                out=w_tile[:].bitcast(I32),
+                out=w_tile[:, :, 0 : 2 * width].bitcast(I32),
                 in_=words_i32[
-                    piece * PIECE : (piece + 1) * PIECE, :, c * CHUNK // 2 : (c + 1) * CHUNK // 2
+                    piece * PIECE : (piece + 1) * PIECE, :, o0 // 2 : (o0 + width) // 2
                 ].rearrange("g p n -> p g n"),
             )
             w_tiles[i] = w_tile
@@ -125,85 +127,98 @@ def tile_yuyipointupdate_pb_k_kernel(tc, h1, w_words, w_scales, g2, b2, out):
                 in_=grouped[:, g0 : g0 + half, :, :].rearrange("p g c t -> p (g c t)"),
             )
 
-        def normalise(c, z_banks):
-            zt_banks = []
-            for u in range(BANKS):
-                z_sb = work.tile([P, BANK], F32, name="z_sb")
-                if u % 2 == 0:
-                    nc.scalar.copy(out=z_sb[:], in_=z_banks[u][:])
-                else:
-                    nc.vector.tensor_copy(out=z_sb[:], in_=z_banks[u][:])
-                zt = psum_zt.tile([P, BLOCKS, P], F32, name="zt")
-                for j in range(BLOCKS):
-                    nc.tensor.transpose(zt[:, j, :], z_sb[:, j * P : (j + 1) * P], ident[:])
-                zt_banks.append(zt)
+        def copy_out_of_psum(bank, dst, src):
+            if bank % 2 == 0:
+                nc.scalar.copy(out=dst, in_=src)
+            else:
+                nc.vector.tensor_copy(out=dst, in_=src)
 
-            stats = small.tile([P, TILES, 6], F32, name="stats")
-            mean_var = small.tile([P, TILES, 2], F32, name="mean_var")
-            for m in range(TILES):
-                nc.vector.bn_stats(out=stats[:, m, :], in_=zt_banks[m // BLOCKS][:, m % BLOCKS, :])
-            for m in range(TILES):
-                nc.vector.bn_aggr(out=mean_var[:, m, :], in_=stats[:, m, :])
-            std = small.tile([P, TILES], F32, name="std")
+        def turn(bank, z):
+            z_sb = work.tile([P, BANK], F32, name="z_sb")
+            copy_out_of_psum(bank, z_sb[:], z[:])
+            zt = psum_zt.tile([P, BLOCKS, P], F32, name="zt")
+            for j in range(BLOCKS):
+                nc.tensor.transpose(zt[:, j, :], z_sb[:, j * P : (j + 1) * P], ident[:])
+            return zt
+
+        def statistics(zt):
+            stats = small.tile([P, BLOCKS, 6], F32, name="stats")
+            mean_var = small.tile([P, BLOCKS, 2], F32, name="mean_var")
+            for j in range(BLOCKS):
+                nc.vector.bn_stats(out=stats[:, j, :], in_=zt[:, j, :])
+            for j in range(BLOCKS):
+                nc.vector.bn_aggr(out=mean_var[:, j, :], in_=stats[:, j, :])
+            return mean_var
+
+        def coefficients(bank, mean_var):
+            m0 = bank * BLOCKS
+            std = small.tile([P, BLOCKS], F32, name="std")
             nc.scalar.activation(out=std[:], in_=mean_var[:, :, 1], func=ACT.Sqrt, bias=eps[:, 0:1], scale=1.0)
-            rstd = small.tile([P, TILES], F32, name="rstd")
+            rstd = small.tile([P, BLOCKS], F32, name="rstd")
             nc.vector.reciprocal(out=rstd[:], in_=std[:])
-            scale = small.tile([P, TILES], F32, name="scale")
-            nc.vector.tensor_tensor(
-                out=scale[:], in0=rstd[:], in1=gain_shift[:, c * TILES : (c + 1) * TILES], op=ALU.mult
-            )
-            mean_scaled = small.tile([P, TILES], F32, name="mean_scaled")
+            scale = small.tile([P, BLOCKS], F32, name="scale")
+            nc.vector.tensor_tensor(out=scale[:], in0=rstd[:], in1=gain_shift[:, m0 : m0 + BLOCKS], op=ALU.mult)
+            mean_scaled = small.tile([P, BLOCKS], F32, name="mean_scaled")
             nc.vector.tensor_tensor(out=mean_scaled[:], in0=mean_var[:, :, 0], in1=scale[:], op=ALU.mult)
-            bias = small.tile([P, TILES], F32, name="bias")
+            bias = small.tile([P, BLOCKS], F32, name="bias")
             nc.vector.tensor_tensor(
-                out=bias[:],
-                in0=gain_shift[:, rows + c * TILES : rows + (c + 1) * TILES],
-                in1=mean_scaled[:],
-                op=ALU.subtract,
+                out=bias[:], in0=gain_shift[:, rows + m0 : rows + m0 + BLOCKS], in1=mean_scaled[:], op=ALU.subtract
             )
-            results = []
-            for u in range(BANKS):
-                y = work.tile([P, BLOCKS, P], F32, name="y")
-                for j in range(BLOCKS):
-                    m = u * BLOCKS + j
-                    nc.scalar.activation(
-                        out=y[:, j, :],
-                        in_=zt_banks[u][:, j, :],
-                        func=ACT.Identity,
-                        bias=bias[:, m : m + 1],
-                        scale=scale[:, m : m + 1],
-                    )
-                r = work.tile([P, BLOCKS, P], F32, name="r")
-                nc.vector.scalar_tensor_tensor(
-                    out=r[:], in0=y[:], scalar=NEG_SLOPE, in1=y[:], op0=ALU.mult, op1=ALU.max
+            return scale, bias
+
+        def apply(zt, scale, bias):
+            y = work.tile([P, BLOCKS, P], F32, name="y")
+            for j in range(BLOCKS):
+                nc.scalar.activation(
+                    out=y[:, j, :],
+                    in_=zt[:, j, :],
+                    func=ACT.Identity,
+                    bias=bias[:, j : j + 1],
+                    scale=scale[:, j : j + 1],
                 )
-                results.append(r)
+            return y
+
+        def leaky_relu(y):
+            r = res_pool.tile([P, BLOCKS, P], F32, name="r")
+            nc.vector.scalar_tensor_tensor(out=r[:], in0=y[:], scalar=NEG_SLOPE, in1=y[:], op0=ALU.mult, op1=ALU.max)
+            return r
+
+        def normalise(banks, z_banks):
+            n = len(banks)
+            zts = [turn(banks[k], z_banks[k]) for k in range(min(2, n))]
+            coeffs = coefficients(banks[0], statistics(zts[0]))
+            results = []
+            for k in range(n):
+                y = apply(zts[k], coeffs[0], coeffs[1])
+                if k + 2 < n:
+                    zts.append(turn(banks[k + 2], z_banks[k + 2]))
+                if k + 1 < n:
+                    mean_var = statistics(zts[k + 1])
+                results.append((banks[k], leaky_relu(y)))
+                if k + 1 < n:
+                    coeffs = coefficients(banks[k + 1], mean_var)
             return results
 
-        def finish(c, results):
-            for u in range(BANKS):
-                rt = psum_rt.tile([P, BANK], F32, name="rt")
-                for j in range(BLOCKS):
-                    nc.tensor.transpose(rt[:, j * P : (j + 1) * P], results[u][:, j, :], ident[:])
-                o_sb = work.tile([P, BANK], F32, name="o_sb")
-                if u % 2 == 0:
-                    nc.scalar.copy(out=o_sb[:], in_=rt[:])
-                else:
-                    nc.vector.tensor_copy(out=o_sb[:], in_=rt[:])
-                o0 = c * CHUNK + u * BANK
-                nc.scalar.dma_start(out=out_rows[:, o0 : o0 + BANK], in_=o_sb[:])
+        def finish(bank, r):
+            rt = psum_rt.tile([P, BANK], F32, name="rt")
+            for j in range(BLOCKS):
+                nc.tensor.transpose(rt[:, j * P : (j + 1) * P], r[:, j, :], ident[:])
+            o_sb = work.tile([P, BANK], F32, name="o_sb")
+            copy_out_of_psum(bank, o_sb[:], rt[:])
+            nc.scalar.dma_start(out=out_rows[:, bank * BANK : (bank + 1) * BANK], in_=o_sb[:])
 
-        results = None
-        for c in range(CHUNKS):
-            z_banks = [psum_z.tile([P, BANK], F32, name="z") for u in range(BANKS)]
+        waiting = []
+        for c in range(len(CHUNK_BANKS)):
+            banks = [first_bank[c] + u for u in range(CHUNK_BANKS[c])]
+            z_banks = [psum_z.tile([P, BANK], F32, name="z") for u in banks]
             for piece in range(PIECES):
                 i = c * PIECES + piece
-                if i + AHEAD < CHUNKS * PIECES:
+                if i + AHEAD < len(CHUNK_BANKS) * PIECES:
                     load_piece(i + AHEAD)
                 w_tile = w_tiles[i]
                 for k in range(PIECE):
                     g = piece * PIECE + k
-                    for u in range(BANKS):
+                    for u in range(CHUNK_BANKS[c]):
                         nc.tensor.matmul_mx(
                             out=z_banks[u][:],
                             lhsT=h_codes[:, g, :].bitcast(FP8X4),
@@ -213,7 +228,8 @@ def tile_yuyipointupdate_pb_k_kernel(tc, h1, w_words, w_scales, g2, b2, out):
                             start=(g == 0),
                             stop=(g == PASSES - 1),
                         )
-                if piece == 0 and c > 0:
-                    finish(c - 1, results)
-            results = normalise(c, z_banks)
-        finish(CHUNKS - 1, results)
+                if piece % 2 == 1 and piece // 2 < len(waiting):
+                    finish(waiting[piece // 2][0], waiting[piece // 2][1])
+            waiting = normalise(banks, z_banks)
+        for bank, r in waiting:
+            finish(bank, r)

@@ -20,8 +20,10 @@ C_OUT = 4096
 PASSES = C_IN // K_PASS
 BANK = 512
 BLOCKS = BANK // P
-CHUNK_BANKS = (4, 2, 2)
-PIECE = 2
+CHUNK = 1024
+BANKS = CHUNK // BANK
+CHUNKS = C_OUT // CHUNK
+PIECE = 4
 PIECES = PASSES // PIECE
 AHEAD = 8
 SCALE_RUN = 8
@@ -36,46 +38,35 @@ def tile_yuyipointupdate_pb_k_kernel(tc, h1, w_words, w_scales, g2, b2, out):
     words_i32 = w_words.bitcast(I32)
     scales_i32 = w_scales.bitcast(I32)
     out_rows = out.rearrange("b n o -> (b n) o")
-    first_bank = [sum(CHUNK_BANKS[:c]) for c in range(len(CHUNK_BANKS))]
-    widest = max(CHUNK_BANKS) * BANK
+    rows = C_OUT // P
 
     with tc.manual_schedule(), tc.tile_pool(name="keep", bufs=1) as keep, tc.tile_pool(
         name="raw", bufs=GRAPHS
     ) as raw_pool, tc.tile_pool(name="weights", bufs=AHEAD + 1) as w_pool, tc.tile_pool(
-        name="work", bufs=3
-    ) as work, tc.tile_pool(name="results", bufs=max(CHUNK_BANKS) + 2) as res_pool, tc.tile_pool(
-        name="small", bufs=3
-    ) as small, tc.psum_pool(name="psum_z", bufs=max(CHUNK_BANKS)) as psum_z, tc.psum_pool(
-        name="psum_zt", bufs=2
-    ) as psum_zt, tc.psum_pool(name="psum_rt", bufs=2) as psum_rt:
+        name="work", bufs=2 * BANKS
+    ) as work, tc.tile_pool(name="small", bufs=3) as small, tc.psum_pool(
+        name="psum_z", bufs=2 * BANKS
+    ) as psum_z, tc.psum_pool(name="psum_zt", bufs=BANKS) as psum_zt, tc.psum_pool(
+        name="psum_rt", bufs=BANKS
+    ) as psum_rt:
         gain_shift_rows = keep.tile([P, P], BF16)
         nc.vector.memset(gain_shift_rows[:], 0.0)
         eps = keep.tile([P, 1], F32)
         nc.vector.memset(eps[:], EPS_BN)
-        rows = C_OUT // P
         nc.scalar.dma_start(out=gain_shift_rows[0:rows, :], in_=g2.rearrange("(m p) -> m p", p=P))
         nc.scalar.dma_start(out=gain_shift_rows[rows : 2 * rows, :], in_=b2.rearrange("(m p) -> m p", p=P))
         ident = keep.tile([P, P], F32)
         make_identity(nc, ident[:])
 
-        planes = []
-        for c in range(len(CHUNK_BANKS)):
-            plane = keep.tile([P, PASSES, CHUNK_BANKS[c] * BANK], U8, name="plane%d" % c, align_bytes=64)
-            nc.vector.memset(plane[:].bitcast(I32), 0)
-            planes.append(plane)
+        planes = {}
 
-        raws = []
-        for b in range(GRAPHS):
-            raw = raw_pool.tile([P, PASSES, PACK, NODES], BF16, name="raw")
-            nc.sync.dma_start(
-                out=raw[:].rearrange("p g t n -> p g (t n)"),
-                in_=h1[b].rearrange("(g p t) n -> p g (t n)", g=PASSES, p=P, t=PACK),
-            )
-            raws.append(raw)
+        def zero_plane(c):
+            plane = keep.tile([P, PASSES, CHUNK], U8, name="plane%d" % c, align_bytes=64)
+            nc.vector.memset(plane[:].bitcast(I32), 0)
+            planes[c] = plane
 
         def load_scales(c):
-            o0 = first_bank[c] * BANK
-            cols = slice(o0 // 4, (o0 + CHUNK_BANKS[c] * BANK) // 4)
+            cols = slice(c * CHUNK // 4, (c + 1) * CHUNK // 4)
             for g0 in range(0, PASSES, SCALE_RUN):
                 for q in range(8):
                     first = 32 * (q // 4) + q % 4
@@ -90,18 +81,25 @@ def tile_yuyipointupdate_pb_k_kernel(tc, h1, w_words, w_scales, g2, b2, out):
             c, piece = divmod(i, PIECES)
             if piece == 0:
                 load_scales(c)
-            o0 = first_bank[c] * BANK
-            width = CHUNK_BANKS[c] * BANK
-            w_tile = w_pool.tile([P, PIECE, 2 * widest], U8, name="w_tile", align_bytes=64)
+            w_tile = w_pool.tile([P, PIECE, 2 * CHUNK], U8, name="w_tile", align_bytes=64)
             nc.sync.dma_start(
-                out=w_tile[:, :, 0 : 2 * width].bitcast(I32),
+                out=w_tile[:].bitcast(I32),
                 in_=words_i32[
-                    piece * PIECE : (piece + 1) * PIECE, :, o0 // 2 : (o0 + width) // 2
+                    piece * PIECE : (piece + 1) * PIECE, :, c * CHUNK // 2 : (c + 1) * CHUNK // 2
                 ].rearrange("g p n -> p g n"),
             )
             w_tiles[i] = w_tile
 
-        for i in range(AHEAD):
+        zero_plane(0)
+        raws = []
+        for b in range(GRAPHS):
+            raw = raw_pool.tile([P, PASSES, PACK, NODES], BF16, name="raw")
+            nc.sync.dma_start(
+                out=raw[:].rearrange("p g t n -> p g (t n)"),
+                in_=h1[b].rearrange("(g p t) n -> p g (t n)", g=PASSES, p=P, t=PACK),
+            )
+            raws.append(raw)
+        for i in range(PIECES):
             load_piece(i)
 
         gain_shift_f32 = keep.tile([P, P], F32)
@@ -127,15 +125,23 @@ def tile_yuyipointupdate_pb_k_kernel(tc, h1, w_words, w_scales, g2, b2, out):
                 in_=grouped[:, g0 : g0 + half, :, :].rearrange("p g c t -> p (g c t)"),
             )
 
+        for c in range(1, CHUNKS):
+            zero_plane(c)
+        for i in range(PIECES, AHEAD):
+            load_piece(i)
+
         def copy_out_of_psum(bank, dst, src):
             if bank % 2 == 0:
                 nc.scalar.copy(out=dst, in_=src)
             else:
                 nc.vector.tensor_copy(out=dst, in_=src)
 
-        def turn(bank, z):
+        def leave(bank, z):
             z_sb = work.tile([P, BANK], F32, name="z_sb")
             copy_out_of_psum(bank, z_sb[:], z[:])
+            return z_sb
+
+        def turn(z_sb):
             zt = psum_zt.tile([P, BLOCKS, P], F32, name="zt")
             for j in range(BLOCKS):
                 nc.tensor.transpose(zt[:, j, :], z_sb[:, j * P : (j + 1) * P], ident[:])
@@ -179,57 +185,62 @@ def tile_yuyipointupdate_pb_k_kernel(tc, h1, w_words, w_scales, g2, b2, out):
             return y
 
         def leaky_relu(y):
-            r = res_pool.tile([P, BLOCKS, P], F32, name="r")
+            r = work.tile([P, BLOCKS, P], F32, name="r")
             nc.vector.scalar_tensor_tensor(out=r[:], in0=y[:], scalar=NEG_SLOPE, in1=y[:], op0=ALU.mult, op1=ALU.max)
             return r
 
-        def normalise(banks, z_banks):
-            n = len(banks)
-            zts = [turn(banks[k], z_banks[k]) for k in range(min(2, n))]
-            coeffs = coefficients(banks[0], statistics(zts[0]))
+        def normalise(c, z_sbs):
+            zts = [turn(z_sb) for z_sb in z_sbs]
+            coeffs = coefficients(c * BANKS, statistics(zts[0]))
             results = []
-            for k in range(n):
-                y = apply(zts[k], coeffs[0], coeffs[1])
-                if k + 2 < n:
-                    zts.append(turn(banks[k + 2], z_banks[k + 2]))
-                if k + 1 < n:
-                    mean_var = statistics(zts[k + 1])
-                results.append((banks[k], leaky_relu(y)))
-                if k + 1 < n:
-                    coeffs = coefficients(banks[k + 1], mean_var)
+            for u in range(BANKS):
+                y = apply(zts[u], coeffs[0], coeffs[1])
+                if u + 1 < BANKS:
+                    mean_var = statistics(zts[u + 1])
+                results.append(leaky_relu(y))
+                if u + 1 < BANKS:
+                    coeffs = coefficients(c * BANKS + u + 1, mean_var)
             return results
 
-        def finish(bank, r):
-            rt = psum_rt.tile([P, BANK], F32, name="rt")
-            for j in range(BLOCKS):
-                nc.tensor.transpose(rt[:, j * P : (j + 1) * P], r[:, j, :], ident[:])
-            o_sb = work.tile([P, BANK], F32, name="o_sb")
-            copy_out_of_psum(bank, o_sb[:], rt[:])
-            nc.scalar.dma_start(out=out_rows[:, bank * BANK : (bank + 1) * BANK], in_=o_sb[:])
+        def finish(c, results):
+            for u in range(BANKS):
+                bank = c * BANKS + u
+                rt = psum_rt.tile([P, BANK], F32, name="rt")
+                for j in range(BLOCKS):
+                    nc.tensor.transpose(rt[:, j * P : (j + 1) * P], results[u][:, j, :], ident[:])
+                o_sb = work.tile([P, BANK], F32, name="o_sb")
+                copy_out_of_psum(bank, o_sb[:], rt[:])
+                nc.scalar.dma_start(out=out_rows[:, bank * BANK : (bank + 1) * BANK], in_=o_sb[:])
 
-        waiting = []
-        for c in range(len(CHUNK_BANKS)):
-            banks = [first_bank[c] + u for u in range(CHUNK_BANKS[c])]
-            z_banks = [psum_z.tile([P, BANK], F32, name="z") for u in banks]
+        z_sbs = {}
+        results = {}
+
+        def transposes_in_chunk(c):
+            if c >= 2:
+                finish(c - 2, results[c - 2])
+            if 1 <= c <= CHUNKS:
+                results[c - 1] = normalise(c - 1, z_sbs[c - 1])
+
+        for c in range(CHUNKS):
+            z_banks = [psum_z.tile([P, BANK], F32, name="z") for u in range(BANKS)]
             for piece in range(PIECES):
                 i = c * PIECES + piece
-                if i + AHEAD < len(CHUNK_BANKS) * PIECES:
+                if i + AHEAD < CHUNKS * PIECES:
                     load_piece(i + AHEAD)
-                w_tile = w_tiles[i]
                 for k in range(PIECE):
                     g = piece * PIECE + k
-                    for u in range(CHUNK_BANKS[c]):
+                    for u in range(BANKS):
                         nc.tensor.matmul_mx(
                             out=z_banks[u][:],
                             lhsT=h_codes[:, g, :].bitcast(FP8X4),
                             lhsT_scale=h_scales[:, g, :],
-                            rhs=w_tile[:, k, 2 * u * BANK : 2 * (u + 1) * BANK].bitcast(FP4X4),
+                            rhs=w_tiles[i][:, k, 2 * u * BANK : 2 * (u + 1) * BANK].bitcast(FP4X4),
                             rhs_scale=planes[c][:, g, u * BANK : (u + 1) * BANK],
                             start=(g == 0),
                             stop=(g == PASSES - 1),
                         )
-                if piece % 2 == 1 and piece // 2 < len(waiting):
-                    finish(waiting[piece // 2][0], waiting[piece // 2][1])
-            waiting = normalise(banks, z_banks)
-        for bank, r in waiting:
-            finish(bank, r)
+                if piece == 0:
+                    transposes_in_chunk(c)
+            z_sbs[c] = [leave(c * BANKS + u, z_banks[u]) for u in range(BANKS)]
+        transposes_in_chunk(CHUNKS)
+        transposes_in_chunk(CHUNKS + 1)

@@ -36,7 +36,6 @@ FLOPS = 2 * GRAPHS * NODES * C_OUT * C_IN
 def tile_yuyipointupdate_pb_k_kernel(tc, h1, w_words, w_scales, g2, b2, out):
     nc = tc.nc
     words_i32 = w_words.bitcast(I32)
-    scales_i32 = w_scales.bitcast(I32)
     out_rows = out.rearrange("b n o -> (b n) o")
     rows = C_OUT // P
 
@@ -66,21 +65,23 @@ def tile_yuyipointupdate_pb_k_kernel(tc, h1, w_words, w_scales, g2, b2, out):
             planes[c] = plane
 
         def load_scales(c):
+            if c == 0:
+                queue, word, run = nc.sync, I32, SCALE_RUN
+            else:
+                queue, word, run = nc.gpsimd, F32, PASSES
             cols = slice(c * CHUNK // 4, (c + 1) * CHUNK // 4)
-            for g0 in range(0, PASSES, SCALE_RUN):
+            for g0 in range(0, PASSES, run):
                 for q in range(8):
                     first = 32 * (q // 4) + q % 4
-                    nc.sync.dma_start(
-                        out=planes[c][first:P:64, g0 : g0 + SCALE_RUN, :].bitcast(I32),
-                        in_=scales_i32[g0 : g0 + SCALE_RUN, q:16:8, cols].rearrange("g q n -> q g n"),
+                    queue.dma_start(
+                        out=planes[c][first:P:64, g0 : g0 + run, :].bitcast(word),
+                        in_=w_scales.bitcast(word)[g0 : g0 + run, q:16:8, cols].rearrange("g q n -> q g n"),
                     )
 
         w_tiles = {}
 
         def load_piece(i):
             c, piece = divmod(i, PIECES)
-            if piece == 0:
-                load_scales(c)
             w_tile = w_pool.tile([P, PIECE, 2 * CHUNK], U8, name="w_tile", align_bytes=64)
             nc.sync.dma_start(
                 out=w_tile[:].bitcast(I32),
@@ -99,6 +100,7 @@ def tile_yuyipointupdate_pb_k_kernel(tc, h1, w_words, w_scales, g2, b2, out):
                 in_=h1[b].rearrange("(g p t) n -> p g (t n)", g=PASSES, p=P, t=PACK),
             )
             raws.append(raw)
+        load_scales(0)
         for i in range(PIECES):
             load_piece(i)
 
@@ -127,6 +129,7 @@ def tile_yuyipointupdate_pb_k_kernel(tc, h1, w_words, w_scales, g2, b2, out):
 
         for c in range(1, CHUNKS):
             zero_plane(c)
+            load_scales(c)
         for i in range(PIECES, AHEAD):
             load_piece(i)
 

@@ -23,9 +23,13 @@ BLOCKS = BANK // P
 CHUNK = 1024
 BANKS = CHUNK // BANK
 CHUNKS = C_OUT // CHUNK
-PIECE = 4
+TILES = CHUNK // P
+PIECE = 2
 PIECES = PASSES // PIECE
-AHEAD = 8
+AHEAD = 16
+TURN_AFTER = 0
+FINISH_AFTER = PIECES - 2
+SCALE_COLS = 2 * CHUNK
 SCALE_RUN = 8
 EPS_BN = 1e-5
 NEG_SLOPE = 0.01
@@ -36,6 +40,7 @@ FLOPS = 2 * GRAPHS * NODES * C_OUT * C_IN
 def tile_yuyipointupdate_pb_k_kernel(tc, h1, w_words, w_scales, g2, b2, out):
     nc = tc.nc
     words_i32 = w_words.bitcast(I32)
+    scales_i32 = w_scales.bitcast(I32)
     out_rows = out.rearrange("b n o -> (b n) o")
     rows = C_OUT // P
 
@@ -43,7 +48,7 @@ def tile_yuyipointupdate_pb_k_kernel(tc, h1, w_words, w_scales, g2, b2, out):
         name="raw", bufs=GRAPHS
     ) as raw_pool, tc.tile_pool(name="weights", bufs=AHEAD + 1) as w_pool, tc.tile_pool(
         name="work", bufs=2 * BANKS
-    ) as work, tc.tile_pool(name="small", bufs=3) as small, tc.psum_pool(
+    ) as work, tc.tile_pool(name="small", bufs=2) as small, tc.psum_pool(
         name="psum_z", bufs=2 * BANKS
     ) as psum_z, tc.psum_pool(name="psum_zt", bufs=BANKS) as psum_zt, tc.psum_pool(
         name="psum_rt", bufs=BANKS
@@ -59,29 +64,27 @@ def tile_yuyipointupdate_pb_k_kernel(tc, h1, w_words, w_scales, g2, b2, out):
 
         planes = {}
 
-        def zero_plane(c):
-            plane = keep.tile([P, PASSES, CHUNK], U8, name="plane%d" % c, align_bytes=64)
+        def zero_planes(s):
+            plane = keep.tile([P, PASSES, SCALE_COLS], U8, name="plane%d" % s, align_bytes=64)
             nc.vector.memset(plane[:].bitcast(I32), 0)
-            planes[c] = plane
+            planes[s] = plane
 
-        def load_scales(c):
-            if c == 0:
-                queue, word, run = nc.sync, I32, SCALE_RUN
-            else:
-                queue, word, run = nc.gpsimd, F32, PASSES
-            cols = slice(c * CHUNK // 4, (c + 1) * CHUNK // 4)
-            for g0 in range(0, PASSES, run):
+        def load_scales(s):
+            cols = slice(s * SCALE_COLS // 4, (s + 1) * SCALE_COLS // 4)
+            for g0 in range(0, PASSES, SCALE_RUN):
                 for q in range(8):
                     first = 32 * (q // 4) + q % 4
-                    queue.dma_start(
-                        out=planes[c][first:P:64, g0 : g0 + run, :].bitcast(word),
-                        in_=w_scales.bitcast(word)[g0 : g0 + run, q:16:8, cols].rearrange("g q n -> q g n"),
+                    nc.sync.dma_start(
+                        out=planes[s][first:P:64, g0 : g0 + SCALE_RUN, :].bitcast(I32),
+                        in_=scales_i32[g0 : g0 + SCALE_RUN, q:16:8, cols].rearrange("g q n -> q g n"),
                     )
 
         w_tiles = {}
 
         def load_piece(i):
             c, piece = divmod(i, PIECES)
+            if piece == 0 and (c * CHUNK) % SCALE_COLS == 0:
+                load_scales(c * CHUNK // SCALE_COLS)
             w_tile = w_pool.tile([P, PIECE, 2 * CHUNK], U8, name="w_tile", align_bytes=64)
             nc.sync.dma_start(
                 out=w_tile[:].bitcast(I32),
@@ -91,7 +94,7 @@ def tile_yuyipointupdate_pb_k_kernel(tc, h1, w_words, w_scales, g2, b2, out):
             )
             w_tiles[i] = w_tile
 
-        zero_plane(0)
+        zero_planes(0)
         raws = []
         for b in range(GRAPHS):
             raw = raw_pool.tile([P, PASSES, PACK, NODES], BF16, name="raw")
@@ -100,8 +103,7 @@ def tile_yuyipointupdate_pb_k_kernel(tc, h1, w_words, w_scales, g2, b2, out):
                 in_=h1[b].rearrange("(g p t) n -> p g (t n)", g=PASSES, p=P, t=PACK),
             )
             raws.append(raw)
-        load_scales(0)
-        for i in range(PIECES):
+        for i in range(AHEAD):
             load_piece(i)
 
         gain_shift_f32 = keep.tile([P, P], F32)
@@ -127,105 +129,99 @@ def tile_yuyipointupdate_pb_k_kernel(tc, h1, w_words, w_scales, g2, b2, out):
                 in_=grouped[:, g0 : g0 + half, :, :].rearrange("p g c t -> p (g c t)"),
             )
 
-        for c in range(1, CHUNKS):
-            zero_plane(c)
-            load_scales(c)
-        for i in range(PIECES, AHEAD):
-            load_piece(i)
+        zero_planes(1)
 
-        def copy_out_of_psum(bank, dst, src):
-            if bank % 2 == 0:
-                nc.scalar.copy(out=dst, in_=src)
-            else:
-                nc.vector.tensor_copy(out=dst, in_=src)
-
-        def leave(bank, z):
-            z_sb = work.tile([P, BANK], F32, name="z_sb")
-            copy_out_of_psum(bank, z_sb[:], z[:])
-            return z_sb
-
-        def turn(z_sb):
-            zt = psum_zt.tile([P, BLOCKS, P], F32, name="zt")
-            for j in range(BLOCKS):
-                nc.tensor.transpose(zt[:, j, :], z_sb[:, j * P : (j + 1) * P], ident[:])
-            return zt
-
-        def statistics(zt):
-            stats = small.tile([P, BLOCKS, 6], F32, name="stats")
-            mean_var = small.tile([P, BLOCKS, 2], F32, name="mean_var")
-            for j in range(BLOCKS):
-                nc.vector.bn_stats(out=stats[:, j, :], in_=zt[:, j, :])
-            for j in range(BLOCKS):
-                nc.vector.bn_aggr(out=mean_var[:, j, :], in_=stats[:, j, :])
-            return mean_var
-
-        def coefficients(bank, mean_var):
-            m0 = bank * BLOCKS
-            std = small.tile([P, BLOCKS], F32, name="std")
-            nc.scalar.activation(out=std[:], in_=mean_var[:, :, 1], func=ACT.Sqrt, bias=eps[:, 0:1], scale=1.0)
-            rstd = small.tile([P, BLOCKS], F32, name="rstd")
-            nc.vector.reciprocal(out=rstd[:], in_=std[:])
-            scale = small.tile([P, BLOCKS], F32, name="scale")
-            nc.vector.tensor_tensor(out=scale[:], in0=rstd[:], in1=gain_shift[:, m0 : m0 + BLOCKS], op=ALU.mult)
-            mean_scaled = small.tile([P, BLOCKS], F32, name="mean_scaled")
-            nc.vector.tensor_tensor(out=mean_scaled[:], in0=mean_var[:, :, 0], in1=scale[:], op=ALU.mult)
-            bias = small.tile([P, BLOCKS], F32, name="bias")
-            nc.vector.tensor_tensor(
-                out=bias[:], in0=gain_shift[:, rows + m0 : rows + m0 + BLOCKS], in1=mean_scaled[:], op=ALU.subtract
-            )
-            return scale, bias
-
-        def apply(zt, scale, bias):
-            y = work.tile([P, BLOCKS, P], F32, name="y")
-            for j in range(BLOCKS):
-                nc.scalar.activation(
-                    out=y[:, j, :],
-                    in_=zt[:, j, :],
-                    func=ACT.Identity,
-                    bias=bias[:, j : j + 1],
-                    scale=scale[:, j : j + 1],
-                )
-            return y
-
-        def leaky_relu(y):
-            r = work.tile([P, BLOCKS, P], F32, name="r")
-            nc.vector.scalar_tensor_tensor(out=r[:], in0=y[:], scalar=NEG_SLOPE, in1=y[:], op0=ALU.mult, op1=ALU.max)
-            return r
+        def leave(z_banks):
+            z_sbs = []
+            for u in range(BANKS):
+                z_sb = work.tile([P, BANK], F32, name="z_sb")
+                if u % 2 == 0:
+                    nc.scalar.copy(out=z_sb[:], in_=z_banks[u][:])
+                else:
+                    nc.vector.tensor_copy(out=z_sb[:], in_=z_banks[u][:])
+                z_sbs.append(z_sb)
+            return z_sbs
 
         def normalise(c, z_sbs):
-            zts = [turn(z_sb) for z_sb in z_sbs]
-            coeffs = coefficients(c * BANKS, statistics(zts[0]))
+            zts = []
+            for u in range(BANKS):
+                zt = psum_zt.tile([P, BLOCKS, P], F32, name="zt")
+                for j in range(BLOCKS):
+                    nc.tensor.transpose(zt[:, j, :], z_sbs[u][:, j * P : (j + 1) * P], ident[:])
+                zts.append(zt)
+
+            stats = small.tile([P, TILES, 6], F32, name="stats")
+            mean_var = small.tile([P, TILES, 2], F32, name="mean_var")
+            for m in range(TILES):
+                nc.vector.bn_stats(out=stats[:, m, :], in_=zts[m // BLOCKS][:, m % BLOCKS, :])
+            for m in range(TILES):
+                nc.vector.bn_aggr(out=mean_var[:, m, :], in_=stats[:, m, :])
+
+            m0 = c * TILES
+            std = small.tile([P, TILES], F32, name="std")
+            nc.scalar.activation(out=std[:], in_=mean_var[:, :, 1], func=ACT.Sqrt, bias=eps[:, 0:1], scale=1.0)
+            rstd = small.tile([P, TILES], F32, name="rstd")
+            nc.vector.reciprocal(out=rstd[:], in_=std[:])
+            scale = small.tile([P, TILES], F32, name="scale")
+            nc.vector.tensor_tensor(out=scale[:], in0=rstd[:], in1=gain_shift[:, m0 : m0 + TILES], op=ALU.mult)
+            mean_scaled = small.tile([P, TILES], F32, name="mean_scaled")
+            nc.vector.tensor_tensor(out=mean_scaled[:], in0=mean_var[:, :, 0], in1=scale[:], op=ALU.mult)
+            bias = small.tile([P, TILES], F32, name="bias")
+            nc.vector.tensor_tensor(
+                out=bias[:], in0=gain_shift[:, rows + m0 : rows + m0 + TILES], in1=mean_scaled[:], op=ALU.subtract
+            )
+
+            ys = []
+            for u in range(BANKS):
+                y = work.tile([P, BLOCKS, P], F32, name="y")
+                for j in range(BLOCKS):
+                    m = u * BLOCKS + j
+                    if u % 2 == 0:
+                        nc.scalar.activation(
+                            out=y[:, j, :],
+                            in_=zts[u][:, j, :],
+                            func=ACT.Identity,
+                            bias=bias[:, m : m + 1],
+                            scale=scale[:, m : m + 1],
+                        )
+                    else:
+                        nc.vector.tensor_scalar(
+                            out=y[:, j, :],
+                            in0=zts[u][:, j, :],
+                            scalar1=scale[:, m : m + 1],
+                            scalar2=bias[:, m : m + 1],
+                            op0=ALU.mult,
+                            op1=ALU.add,
+                        )
+                ys.append(y)
             results = []
             for u in range(BANKS):
-                y = apply(zts[u], coeffs[0], coeffs[1])
-                if u + 1 < BANKS:
-                    mean_var = statistics(zts[u + 1])
-                results.append(leaky_relu(y))
-                if u + 1 < BANKS:
-                    coeffs = coefficients(c * BANKS + u + 1, mean_var)
+                r = work.tile([P, BLOCKS, P], F32, name="r")
+                nc.vector.scalar_tensor_tensor(
+                    out=r[:], in0=ys[u][:], scalar=NEG_SLOPE, in1=ys[u][:], op0=ALU.mult, op1=ALU.max
+                )
+                results.append(r)
             return results
 
         def finish(c, results):
             for u in range(BANKS):
-                bank = c * BANKS + u
                 rt = psum_rt.tile([P, BANK], F32, name="rt")
                 for j in range(BLOCKS):
                     nc.tensor.transpose(rt[:, j * P : (j + 1) * P], results[u][:, j, :], ident[:])
                 o_sb = work.tile([P, BANK], F32, name="o_sb")
-                copy_out_of_psum(bank, o_sb[:], rt[:])
-                nc.scalar.dma_start(out=out_rows[:, bank * BANK : (bank + 1) * BANK], in_=o_sb[:])
+                if u % 2 == 0:
+                    nc.scalar.copy(out=o_sb[:], in_=rt[:])
+                else:
+                    nc.vector.tensor_copy(out=o_sb[:], in_=rt[:])
+                o0 = c * CHUNK + u * BANK
+                nc.scalar.dma_start(out=out_rows[:, o0 : o0 + BANK], in_=o_sb[:])
 
-        z_sbs = {}
-        results = {}
-
-        def transposes_in_chunk(c):
-            if c >= 2:
-                finish(c - 2, results[c - 2])
-            if 1 <= c <= CHUNKS:
-                results[c - 1] = normalise(c - 1, z_sbs[c - 1])
-
+        z_sbs = None
+        results = None
         for c in range(CHUNKS):
             z_banks = [psum_z.tile([P, BANK], F32, name="z") for u in range(BANKS)]
+            plane = planes[c * CHUNK // SCALE_COLS]
+            plane_col = c * CHUNK % SCALE_COLS
             for piece in range(PIECES):
                 i = c * PIECES + piece
                 if i + AHEAD < CHUNKS * PIECES:
@@ -238,12 +234,13 @@ def tile_yuyipointupdate_pb_k_kernel(tc, h1, w_words, w_scales, g2, b2, out):
                             lhsT=h_codes[:, g, :].bitcast(FP8X4),
                             lhsT_scale=h_scales[:, g, :],
                             rhs=w_tiles[i][:, k, 2 * u * BANK : 2 * (u + 1) * BANK].bitcast(FP4X4),
-                            rhs_scale=planes[c][:, g, u * BANK : (u + 1) * BANK],
+                            rhs_scale=plane[:, g, plane_col + u * BANK : plane_col + (u + 1) * BANK],
                             start=(g == 0),
                             stop=(g == PASSES - 1),
                         )
-                if piece == 0:
-                    transposes_in_chunk(c)
-            z_sbs[c] = [leave(c * BANKS + u, z_banks[u]) for u in range(BANKS)]
-        transposes_in_chunk(CHUNKS)
-        transposes_in_chunk(CHUNKS + 1)
+                if c > 0 and piece == TURN_AFTER:
+                    results = normalise(c - 1, z_sbs)
+                if c > 0 and piece == FINISH_AFTER:
+                    finish(c - 1, results)
+            z_sbs = leave(z_banks)
+        finish(CHUNKS - 1, normalise(CHUNKS - 1, z_sbs))

@@ -24,13 +24,11 @@ CHUNK = 1024
 BANKS = CHUNK // BANK
 CHUNKS = C_OUT // CHUNK
 TILES = CHUNK // P
-PIECE = 2
-PIECES = PASSES // PIECE
-AHEAD = 16
-TURN_AFTER = 0
-FINISH_AFTER = PIECES - 2
+PIECE = 4
+LAST_PIECE = 2
+AHEAD = 8
+TURN_AT = 4
 SCALE_COLS = 2 * CHUNK
-SCALE_RUN = 8
 EPS_BN = 1e-5
 NEG_SLOPE = 0.01
 
@@ -40,7 +38,7 @@ FLOPS = 2 * GRAPHS * NODES * C_OUT * C_IN
 def tile_yuyipointupdate_pb_k_kernel(tc, h1, w_words, w_scales, g2, b2, out):
     nc = tc.nc
     words_i32 = w_words.bitcast(I32)
-    scales_i32 = w_scales.bitcast(I32)
+    scales_f32 = w_scales.bitcast(F32)
     out_rows = out.rearrange("b n o -> (b n) o")
     rows = C_OUT // P
 
@@ -71,30 +69,31 @@ def tile_yuyipointupdate_pb_k_kernel(tc, h1, w_words, w_scales, g2, b2, out):
 
         def load_scales(s):
             cols = slice(s * SCALE_COLS // 4, (s + 1) * SCALE_COLS // 4)
-            for g0 in range(0, PASSES, SCALE_RUN):
-                for q in range(8):
-                    first = 32 * (q // 4) + q % 4
-                    nc.sync.dma_start(
-                        out=planes[s][first:P:64, g0 : g0 + SCALE_RUN, :].bitcast(I32),
-                        in_=scales_i32[g0 : g0 + SCALE_RUN, q:16:8, cols].rearrange("g q n -> q g n"),
-                    )
+            for q in range(8):
+                first = 32 * (q // 4) + q % 4
+                nc.gpsimd.dma_start(
+                    out=planes[s][first:P:64, :, :].bitcast(F32),
+                    in_=scales_f32[:, q:16:8, cols].rearrange("g q n -> q g n"),
+                )
 
+        pieces = []
+        for c in range(CHUNKS):
+            n_passes = PIECE if c < CHUNKS - 1 else LAST_PIECE
+            for g0 in range(0, PASSES, n_passes):
+                pieces.append((c, g0, n_passes))
         w_tiles = {}
 
         def load_piece(i):
-            c, piece = divmod(i, PIECES)
-            if piece == 0 and (c * CHUNK) % SCALE_COLS == 0:
-                load_scales(c * CHUNK // SCALE_COLS)
+            c, g0, n_passes = pieces[i]
             w_tile = w_pool.tile([P, PIECE, 2 * CHUNK], U8, name="w_tile", align_bytes=64)
             nc.sync.dma_start(
-                out=w_tile[:].bitcast(I32),
-                in_=words_i32[
-                    piece * PIECE : (piece + 1) * PIECE, :, c * CHUNK // 2 : (c + 1) * CHUNK // 2
-                ].rearrange("g p n -> p g n"),
+                out=w_tile[:, 0:n_passes, :].bitcast(I32),
+                in_=words_i32[g0 : g0 + n_passes, :, c * CHUNK // 2 : (c + 1) * CHUNK // 2].rearrange("g p n -> p g n"),
             )
             w_tiles[i] = w_tile
 
         zero_planes(0)
+        load_scales(0)
         raws = []
         for b in range(GRAPHS):
             raw = raw_pool.tile([P, PASSES, PACK, NODES], BF16, name="raw")
@@ -106,16 +105,9 @@ def tile_yuyipointupdate_pb_k_kernel(tc, h1, w_words, w_scales, g2, b2, out):
         for i in range(AHEAD):
             load_piece(i)
 
-        gain_shift_f32 = keep.tile([P, P], F32)
-        nc.vector.tensor_copy(out=gain_shift_f32[:], in_=gain_shift_rows[:])
-        gs_ps = psum_zt.tile([P, BLOCKS, P], F32, name="zt")
-        nc.tensor.transpose(gs_ps[:, 0, :], gain_shift_f32[:], ident[:])
-        gain_shift = keep.tile([P, 2 * rows], F32)
-        nc.vector.tensor_copy(out=gain_shift[:], in_=gs_ps[:, 0, 0 : 2 * rows])
-
         grouped = keep.tile([P, PASSES, P, PACK], BF16, align_bytes=64)
         for b in range(GRAPHS):
-            nc.vector.tensor_copy(
+            nc.scalar.copy(
                 out=grouped[:, :, b * NODES : (b + 1) * NODES, :],
                 in_=raws[b][:].rearrange("p g t n -> p g n t"),
             )
@@ -130,6 +122,14 @@ def tile_yuyipointupdate_pb_k_kernel(tc, h1, w_words, w_scales, g2, b2, out):
             )
 
         zero_planes(1)
+        load_scales(1)
+
+        gain_shift_f32 = keep.tile([P, P], F32)
+        nc.scalar.copy(out=gain_shift_f32[:], in_=gain_shift_rows[:])
+        gs_ps = psum_zt.tile([P, BLOCKS, P], F32, name="zt")
+        nc.tensor.transpose(gs_ps[:, 0, :], gain_shift_f32[:], ident[:])
+        gain_shift = keep.tile([P, 2 * rows], F32)
+        nc.scalar.copy(out=gain_shift[:], in_=gs_ps[:, 0, 0 : 2 * rows])
 
         def leave(z_banks):
             z_sbs = []
@@ -216,31 +216,33 @@ def tile_yuyipointupdate_pb_k_kernel(tc, h1, w_words, w_scales, g2, b2, out):
                 o0 = c * CHUNK + u * BANK
                 nc.scalar.dma_start(out=out_rows[:, o0 : o0 + BANK], in_=o_sb[:])
 
+        z_banks = None
         z_sbs = None
         results = None
-        for c in range(CHUNKS):
-            z_banks = [psum_z.tile([P, BANK], F32, name="z") for u in range(BANKS)]
+        for i in range(len(pieces)):
+            c, g0, n_passes = pieces[i]
+            if g0 == 0:
+                z_banks = [psum_z.tile([P, BANK], F32, name="z") for u in range(BANKS)]
+            if i + AHEAD < len(pieces):
+                load_piece(i + AHEAD)
             plane = planes[c * CHUNK // SCALE_COLS]
             plane_col = c * CHUNK % SCALE_COLS
-            for piece in range(PIECES):
-                i = c * PIECES + piece
-                if i + AHEAD < CHUNKS * PIECES:
-                    load_piece(i + AHEAD)
-                for k in range(PIECE):
-                    g = piece * PIECE + k
-                    for u in range(BANKS):
-                        nc.tensor.matmul_mx(
-                            out=z_banks[u][:],
-                            lhsT=h_codes[:, g, :].bitcast(FP8X4),
-                            lhsT_scale=h_scales[:, g, :],
-                            rhs=w_tiles[i][:, k, 2 * u * BANK : 2 * (u + 1) * BANK].bitcast(FP4X4),
-                            rhs_scale=plane[:, g, plane_col + u * BANK : plane_col + (u + 1) * BANK],
-                            start=(g == 0),
-                            stop=(g == PASSES - 1),
-                        )
-                if c > 0 and piece == TURN_AFTER:
-                    results = normalise(c - 1, z_sbs)
-                if c > 0 and piece == FINISH_AFTER:
+            for k in range(n_passes):
+                g = g0 + k
+                for u in range(BANKS):
+                    nc.tensor.matmul_mx(
+                        out=z_banks[u][:],
+                        lhsT=h_codes[:, g, :].bitcast(FP8X4),
+                        lhsT_scale=h_scales[:, g, :],
+                        rhs=w_tiles[i][:, k, 2 * u * BANK : 2 * (u + 1) * BANK].bitcast(FP4X4),
+                        rhs_scale=plane[:, g, plane_col + u * BANK : plane_col + (u + 1) * BANK],
+                        start=(g == 0),
+                        stop=(g == PASSES - 1),
+                    )
+            if c > 0 and g0 + n_passes == TURN_AT:
+                results = normalise(c - 1, z_sbs)
+            if g0 + n_passes == PASSES:
+                z_sbs = leave(z_banks)
+                if c > 0:
                     finish(c - 1, results)
-            z_sbs = leave(z_banks)
         finish(CHUNKS - 1, normalise(CHUNKS - 1, z_sbs))

@@ -28,7 +28,7 @@ PIECE = 4
 LAST_PIECE = 2
 AHEAD = 8
 TURN_AT = 4
-SCALE_COLS = 2 * CHUNK
+SCALE_RUN = 8
 EPS_BN = 1e-5
 NEG_SLOPE = 0.01
 
@@ -38,7 +38,7 @@ FLOPS = 2 * GRAPHS * NODES * C_OUT * C_IN
 def tile_yuyipointupdate_pb_k_kernel(tc, h1, w_words, w_scales, g2, b2, out):
     nc = tc.nc
     words_i32 = w_words.bitcast(I32)
-    scales_f32 = w_scales.bitcast(F32)
+    scales_i32 = w_scales.bitcast(I32)
     out_rows = out.rearrange("b n o -> (b n) o")
     rows = C_OUT // P
 
@@ -62,19 +62,20 @@ def tile_yuyipointupdate_pb_k_kernel(tc, h1, w_words, w_scales, g2, b2, out):
 
         planes = {}
 
-        def zero_planes(s):
-            plane = keep.tile([P, PASSES, SCALE_COLS], U8, name="plane%d" % s, align_bytes=64)
+        def zero_plane(c):
+            plane = keep.tile([P, PASSES, CHUNK], U8, name="plane%d" % c, align_bytes=64)
             nc.vector.memset(plane[:].bitcast(I32), 0)
-            planes[s] = plane
+            planes[c] = plane
 
-        def load_scales(s):
-            cols = slice(s * SCALE_COLS // 4, (s + 1) * SCALE_COLS // 4)
-            for q in range(8):
-                first = 32 * (q // 4) + q % 4
-                nc.gpsimd.dma_start(
-                    out=planes[s][first:P:64, :, :].bitcast(F32),
-                    in_=scales_f32[:, q:16:8, cols].rearrange("g q n -> q g n"),
-                )
+        def load_scales(c):
+            cols = slice(c * CHUNK // 4, (c + 1) * CHUNK // 4)
+            for g0 in range(0, PASSES, SCALE_RUN):
+                for q in range(8):
+                    first = 32 * (q // 4) + q % 4
+                    nc.sync.dma_start(
+                        out=planes[c][first:P:64, g0 : g0 + SCALE_RUN, :].bitcast(I32),
+                        in_=scales_i32[g0 : g0 + SCALE_RUN, q:16:8, cols].rearrange("g q n -> q g n"),
+                    )
 
         pieces = []
         for c in range(CHUNKS):
@@ -85,6 +86,8 @@ def tile_yuyipointupdate_pb_k_kernel(tc, h1, w_words, w_scales, g2, b2, out):
 
         def load_piece(i):
             c, g0, n_passes = pieces[i]
+            if g0 == 0:
+                load_scales(c)
             w_tile = w_pool.tile([P, PIECE, 2 * CHUNK], U8, name="w_tile", align_bytes=64)
             nc.sync.dma_start(
                 out=w_tile[:, 0:n_passes, :].bitcast(I32),
@@ -92,8 +95,7 @@ def tile_yuyipointupdate_pb_k_kernel(tc, h1, w_words, w_scales, g2, b2, out):
             )
             w_tiles[i] = w_tile
 
-        zero_planes(0)
-        load_scales(0)
+        zero_plane(0)
         raws = []
         for b in range(GRAPHS):
             raw = raw_pool.tile([P, PASSES, PACK, NODES], BF16, name="raw")
@@ -102,12 +104,20 @@ def tile_yuyipointupdate_pb_k_kernel(tc, h1, w_words, w_scales, g2, b2, out):
                 in_=h1[b].rearrange("(g p t) n -> p g (t n)", g=PASSES, p=P, t=PACK),
             )
             raws.append(raw)
-        for i in range(AHEAD):
+        first_loads = PASSES // PIECE
+        for i in range(first_loads):
             load_piece(i)
+
+        gain_shift_f32 = keep.tile([P, P], F32)
+        nc.scalar.copy(out=gain_shift_f32[:], in_=gain_shift_rows[:])
+        gs_ps = psum_zt.tile([P, BLOCKS, P], F32, name="zt")
+        nc.tensor.transpose(gs_ps[:, 0, :], gain_shift_f32[:], ident[:])
+        gain_shift = keep.tile([P, 2 * rows], F32)
+        nc.scalar.copy(out=gain_shift[:], in_=gs_ps[:, 0, 0 : 2 * rows])
 
         grouped = keep.tile([P, PASSES, P, PACK], BF16, align_bytes=64)
         for b in range(GRAPHS):
-            nc.scalar.copy(
+            nc.vector.tensor_copy(
                 out=grouped[:, :, b * NODES : (b + 1) * NODES, :],
                 in_=raws[b][:].rearrange("p g t n -> p g n t"),
             )
@@ -121,15 +131,10 @@ def tile_yuyipointupdate_pb_k_kernel(tc, h1, w_words, w_scales, g2, b2, out):
                 in_=grouped[:, g0 : g0 + half, :, :].rearrange("p g c t -> p (g c t)"),
             )
 
-        zero_planes(1)
-        load_scales(1)
-
-        gain_shift_f32 = keep.tile([P, P], F32)
-        nc.scalar.copy(out=gain_shift_f32[:], in_=gain_shift_rows[:])
-        gs_ps = psum_zt.tile([P, BLOCKS, P], F32, name="zt")
-        nc.tensor.transpose(gs_ps[:, 0, :], gain_shift_f32[:], ident[:])
-        gain_shift = keep.tile([P, 2 * rows], F32)
-        nc.scalar.copy(out=gain_shift[:], in_=gs_ps[:, 0, 0 : 2 * rows])
+        for c in range(1, CHUNKS):
+            zero_plane(c)
+        for i in range(first_loads, AHEAD):
+            load_piece(i)
 
         def leave(z_banks):
             z_sbs = []
@@ -203,18 +208,26 @@ def tile_yuyipointupdate_pb_k_kernel(tc, h1, w_words, w_scales, g2, b2, out):
                 results.append(r)
             return results
 
+        o_all = keep.tile([P, C_OUT], F32)
+        to_store = []
+        stored = [0]
+
         def finish(c, results):
             for u in range(BANKS):
                 rt = psum_rt.tile([P, BANK], F32, name="rt")
                 for j in range(BLOCKS):
                     nc.tensor.transpose(rt[:, j * P : (j + 1) * P], results[u][:, j, :], ident[:])
-                o_sb = work.tile([P, BANK], F32, name="o_sb")
-                if u % 2 == 0:
-                    nc.scalar.copy(out=o_sb[:], in_=rt[:])
-                else:
-                    nc.vector.tensor_copy(out=o_sb[:], in_=rt[:])
                 o0 = c * CHUNK + u * BANK
-                nc.scalar.dma_start(out=out_rows[:, o0 : o0 + BANK], in_=o_sb[:])
+                if u % 2 == 0:
+                    nc.scalar.copy(out=o_all[:, o0 : o0 + BANK], in_=rt[:])
+                else:
+                    nc.vector.tensor_copy(out=o_all[:, o0 : o0 + BANK], in_=rt[:])
+                to_store.append(o0)
+
+        def store_what_is_ready():
+            for o0 in to_store[stored[0] :]:
+                nc.sync.dma_start(out=out_rows[:, o0 : o0 + BANK], in_=o_all[:, o0 : o0 + BANK])
+            stored[0] = len(to_store)
 
         z_banks = None
         z_sbs = None
@@ -225,8 +238,8 @@ def tile_yuyipointupdate_pb_k_kernel(tc, h1, w_words, w_scales, g2, b2, out):
                 z_banks = [psum_z.tile([P, BANK], F32, name="z") for u in range(BANKS)]
             if i + AHEAD < len(pieces):
                 load_piece(i + AHEAD)
-            plane = planes[c * CHUNK // SCALE_COLS]
-            plane_col = c * CHUNK % SCALE_COLS
+            else:
+                store_what_is_ready()
             for k in range(n_passes):
                 g = g0 + k
                 for u in range(BANKS):
@@ -235,7 +248,7 @@ def tile_yuyipointupdate_pb_k_kernel(tc, h1, w_words, w_scales, g2, b2, out):
                         lhsT=h_codes[:, g, :].bitcast(FP8X4),
                         lhsT_scale=h_scales[:, g, :],
                         rhs=w_tiles[i][:, k, 2 * u * BANK : 2 * (u + 1) * BANK].bitcast(FP4X4),
-                        rhs_scale=plane[:, g, plane_col + u * BANK : plane_col + (u + 1) * BANK],
+                        rhs_scale=planes[c][:, g, u * BANK : (u + 1) * BANK],
                         start=(g == 0),
                         stop=(g == PASSES - 1),
                     )
@@ -245,4 +258,6 @@ def tile_yuyipointupdate_pb_k_kernel(tc, h1, w_words, w_scales, g2, b2, out):
                 z_sbs = leave(z_banks)
                 if c > 0:
                     finish(c - 1, results)
+        store_what_is_ready()
         finish(CHUNKS - 1, normalise(CHUNKS - 1, z_sbs))
+        store_what_is_ready()

@@ -28,7 +28,7 @@ PIECE = 4
 LAST_PIECE = 2
 AHEAD = 8
 TURN_AT = 4
-SCALE_RUN = 8
+SCALE_RUN = 4
 EPS_BN = 1e-5
 NEG_SLOPE = 0.01
 
@@ -70,11 +70,10 @@ def tile_yuyipointupdate_pb_k_kernel(tc, h1, w_words, w_scales, g2, b2, out):
         def load_scales(c):
             cols = slice(c * CHUNK // 4, (c + 1) * CHUNK // 4)
             for g0 in range(0, PASSES, SCALE_RUN):
-                for q in range(8):
-                    first = 32 * (q // 4) + q % 4
+                for r in range(4):
                     nc.sync.dma_start(
-                        out=planes[c][first:P:64, g0 : g0 + SCALE_RUN, :].bitcast(I32),
-                        in_=scales_i32[g0 : g0 + SCALE_RUN, q:16:8, cols].rearrange("g q n -> q g n"),
+                        out=planes[c][r:P:32, g0 : g0 + SCALE_RUN, :].bitcast(I32),
+                        in_=scales_i32[g0 : g0 + SCALE_RUN, r:16:4, cols].rearrange("g q n -> q g n"),
                     )
 
         pieces = []

@@ -19,15 +19,12 @@ C_IN = 8192
 C_OUT = 4096
 PASSES = C_IN // K_PASS
 BANK = 512
-BLOCKS = BANK // P
-CHUNK = 1024
-BANKS = CHUNK // BANK
-CHUNKS = C_OUT // CHUNK
-TILES = CHUNK // P
-PIECE = 4
-LAST_PIECE = 2
+PLANE = 1024
+CHUNK_BANKS = (2, 2, 2, 1, 1)
+CHUNK_PIECES = ((4, 4, 4, 4), (4, 4, 4, 4), (4, 4, 4, 4), (4, 4, 4, 4), (4, 4, 4, 2, 2))
+SIDES = 2
 AHEAD = 8
-TURN_AT = 4
+BACK_AT = 8
 SCALE_RUN = 4
 EPS_BN = 1e-5
 NEG_SLOPE = 0.01
@@ -41,15 +38,17 @@ def tile_yuyipointupdate_pb_k_kernel(tc, h1, w_words, w_scales, g2, b2, out):
     scales_i32 = w_scales.bitcast(I32)
     out_rows = out.rearrange("b n o -> (b n) o")
     rows = C_OUT // P
+    chunks = len(CHUNK_BANKS)
+    first_col = [BANK * sum(CHUNK_BANKS[:c]) for c in range(chunks)]
 
     with tc.manual_schedule(), tc.tile_pool(name="keep", bufs=1) as keep, tc.tile_pool(
         name="raw", bufs=GRAPHS
     ) as raw_pool, tc.tile_pool(name="weights", bufs=AHEAD + 1) as w_pool, tc.tile_pool(
-        name="work", bufs=2 * BANKS
+        name="work", bufs=2 * SIDES
     ) as work, tc.tile_pool(name="small", bufs=2) as small, tc.psum_pool(
-        name="psum_z", bufs=2 * BANKS
-    ) as psum_z, tc.psum_pool(name="psum_zt", bufs=BANKS) as psum_zt, tc.psum_pool(
-        name="psum_rt", bufs=BANKS
+        name="psum_z", bufs=4
+    ) as psum_z, tc.psum_pool(name="psum_zt", bufs=SIDES) as psum_zt, tc.psum_pool(
+        name="psum_rt", bufs=SIDES
     ) as psum_rt:
         gain_shift_rows = keep.tile([P, P], BF16)
         nc.vector.memset(gain_shift_rows[:], 0.0)
@@ -62,35 +61,39 @@ def tile_yuyipointupdate_pb_k_kernel(tc, h1, w_words, w_scales, g2, b2, out):
 
         planes = {}
 
-        def zero_plane(c):
-            plane = keep.tile([P, PASSES, CHUNK], U8, name="plane%d" % c, align_bytes=64)
+        def zero_plane(s):
+            plane = keep.tile([P, PASSES, PLANE], U8, name="plane%d" % s, align_bytes=64)
             nc.vector.memset(plane[:].bitcast(I32), 0)
-            planes[c] = plane
+            planes[s] = plane
 
-        def load_scales(c):
-            cols = slice(c * CHUNK // 4, (c + 1) * CHUNK // 4)
+        def load_scales(s):
+            cols = slice(s * PLANE // 4, (s + 1) * PLANE // 4)
             for g0 in range(0, PASSES, SCALE_RUN):
                 for r in range(4):
                     nc.sync.dma_start(
-                        out=planes[c][r:P:32, g0 : g0 + SCALE_RUN, :].bitcast(I32),
+                        out=planes[s][r:P:32, g0 : g0 + SCALE_RUN, :].bitcast(I32),
                         in_=scales_i32[g0 : g0 + SCALE_RUN, r:16:4, cols].rearrange("g q n -> q g n"),
                     )
 
         pieces = []
-        for c in range(CHUNKS):
-            n_passes = PIECE if c < CHUNKS - 1 else LAST_PIECE
-            for g0 in range(0, PASSES, n_passes):
+        for c in range(chunks):
+            g0 = 0
+            for n_passes in CHUNK_PIECES[c]:
                 pieces.append((c, g0, n_passes))
+                g0 += n_passes
         w_tiles = {}
 
         def load_piece(i):
             c, g0, n_passes = pieces[i]
-            if g0 == 0:
-                load_scales(c)
-            w_tile = w_pool.tile([P, PIECE, 2 * CHUNK], U8, name="w_tile", align_bytes=64)
+            if g0 == 0 and first_col[c] % PLANE == 0:
+                load_scales(first_col[c] // PLANE)
+            width = BANK * CHUNK_BANKS[c]
+            w_tile = w_pool.tile([P, n_passes, 2 * width], U8, name="w_tile", align_bytes=64)
             nc.sync.dma_start(
-                out=w_tile[:, 0:n_passes, :].bitcast(I32),
-                in_=words_i32[g0 : g0 + n_passes, :, c * CHUNK // 2 : (c + 1) * CHUNK // 2].rearrange("g p n -> p g n"),
+                out=w_tile[:].bitcast(I32),
+                in_=words_i32[g0 : g0 + n_passes, :, first_col[c] // 2 : (first_col[c] + width) // 2].rearrange(
+                    "g p n -> p g n"
+                ),
             )
             w_tiles[i] = w_tile
 
@@ -103,16 +106,16 @@ def tile_yuyipointupdate_pb_k_kernel(tc, h1, w_words, w_scales, g2, b2, out):
                 in_=h1[b].rearrange("(g p t) n -> p g (t n)", g=PASSES, p=P, t=PACK),
             )
             raws.append(raw)
-        first_loads = PASSES // PIECE
+        first_loads = len(CHUNK_PIECES[0])
         for i in range(first_loads):
             load_piece(i)
 
         gain_shift_f32 = keep.tile([P, P], F32)
         nc.scalar.copy(out=gain_shift_f32[:], in_=gain_shift_rows[:])
-        gs_ps = psum_zt.tile([P, BLOCKS, P], F32, name="zt")
-        nc.tensor.transpose(gs_ps[:, 0, :], gain_shift_f32[:], ident[:])
+        gs_ps = psum_zt.tile([P, BANK], F32, name="zt")
+        nc.tensor.transpose(gs_ps[:, 0:P], gain_shift_f32[:], ident[:])
         gain_shift = keep.tile([P, 2 * rows], F32)
-        nc.scalar.copy(out=gain_shift[:], in_=gs_ps[:, 0, 0 : 2 * rows])
+        nc.scalar.copy(out=gain_shift[:], in_=gs_ps[:, 0 : 2 * rows])
 
         grouped = keep.tile([P, PASSES, P, PACK], BF16, align_bytes=64)
         for b in range(GRAPHS):
@@ -130,79 +133,94 @@ def tile_yuyipointupdate_pb_k_kernel(tc, h1, w_words, w_scales, g2, b2, out):
                 in_=grouped[:, g0 : g0 + half, :, :].rearrange("p g c t -> p (g c t)"),
             )
 
-        for c in range(1, CHUNKS):
-            zero_plane(c)
+        for s in range(1, C_OUT // PLANE):
+            zero_plane(s)
         for i in range(first_loads, AHEAD):
             load_piece(i)
 
-        def leave(z_banks):
+        def leave(c, z_banks, vector_helps=True):
+            side_cols = BANK * CHUNK_BANKS[c] // SIDES
             z_sbs = []
-            for u in range(BANKS):
-                z_sb = work.tile([P, BANK], F32, name="z_sb")
-                if u % 2 == 0:
-                    nc.scalar.copy(out=z_sb[:], in_=z_banks[u][:])
+            for s in range(SIDES):
+                z_sb = work.tile([P, side_cols], F32, name="z_sb")
+                src_bank = z_banks[s * side_cols // BANK]
+                lo = s * side_cols % BANK
+                if s == 0 or len(z_banks) == 1 or not vector_helps:
+                    nc.scalar.copy(out=z_sb[:], in_=src_bank[:, lo : lo + side_cols])
                 else:
-                    nc.vector.tensor_copy(out=z_sb[:], in_=z_banks[u][:])
+                    nc.vector.tensor_copy(out=z_sb[:], in_=src_bank[:, lo : lo + side_cols])
                 z_sbs.append(z_sb)
             return z_sbs
 
-        def normalise(c, z_sbs):
+        def turn(c, z_sbs):
+            blocks = BANK * CHUNK_BANKS[c] // SIDES // P
             zts = []
-            for u in range(BANKS):
-                zt = psum_zt.tile([P, BLOCKS, P], F32, name="zt")
-                for j in range(BLOCKS):
-                    nc.tensor.transpose(zt[:, j, :], z_sbs[u][:, j * P : (j + 1) * P], ident[:])
+            for z_sb in z_sbs:
+                if c == chunks - 2:
+                    zt = psum_z.tile([P, BANK], F32, name="z")
+                else:
+                    zt = psum_zt.tile([P, BANK], F32, name="zt")
+                for j in range(blocks):
+                    nc.tensor.transpose(zt[:, j * P : (j + 1) * P], z_sb[:, j * P : (j + 1) * P], ident[:])
                 zts.append(zt)
+            return zts
 
-            stats = small.tile([P, TILES, 6], F32, name="stats")
-            mean_var = small.tile([P, TILES, 2], F32, name="mean_var")
-            for m in range(TILES):
-                nc.vector.bn_stats(out=stats[:, m, :], in_=zts[m // BLOCKS][:, m % BLOCKS, :])
-            for m in range(TILES):
+        def normalise(c, zts, vector_helps=True):
+            blocks = BANK * CHUNK_BANKS[c] // SIDES // P
+            tiles = SIDES * blocks
+            stats = small.tile([P, tiles, 6], F32, name="stats")
+            mean_var = small.tile([P, tiles, 2], F32, name="mean_var")
+            for m in range(tiles):
+                nc.vector.bn_stats(out=stats[:, m, :], in_=zts[m // blocks][:, (m % blocks) * P : (m % blocks + 1) * P])
+            for m in range(tiles):
                 nc.vector.bn_aggr(out=mean_var[:, m, :], in_=stats[:, m, :])
 
-            m0 = c * TILES
-            std = small.tile([P, TILES], F32, name="std")
+            m0 = first_col[c] // P
+            std = small.tile([P, tiles], F32, name="std")
             nc.scalar.activation(out=std[:], in_=mean_var[:, :, 1], func=ACT.Sqrt, bias=eps[:, 0:1], scale=1.0)
-            rstd = small.tile([P, TILES], F32, name="rstd")
+            centred = []
+            for s in range(SIDES):
+                zc = work.tile([P, blocks * P], F32, name="zc")
+                for j in range(blocks):
+                    m = s * blocks + j
+                    nc.vector.tensor_scalar_sub(
+                        out=zc[:, j * P : (j + 1) * P], in0=zts[s][:, j * P : (j + 1) * P], scalar1=mean_var[:, m, 0:1]
+                    )
+                centred.append(zc)
+            rstd = small.tile([P, tiles], F32, name="rstd")
             nc.vector.reciprocal(out=rstd[:], in_=std[:])
-            scale = small.tile([P, TILES], F32, name="scale")
-            nc.vector.tensor_tensor(out=scale[:], in0=rstd[:], in1=gain_shift[:, m0 : m0 + TILES], op=ALU.mult)
-            mean_scaled = small.tile([P, TILES], F32, name="mean_scaled")
-            nc.vector.tensor_tensor(out=mean_scaled[:], in0=mean_var[:, :, 0], in1=scale[:], op=ALU.mult)
-            bias = small.tile([P, TILES], F32, name="bias")
-            nc.vector.tensor_tensor(
-                out=bias[:], in0=gain_shift[:, rows + m0 : rows + m0 + TILES], in1=mean_scaled[:], op=ALU.subtract
-            )
+            scale = small.tile([P, tiles], F32, name="scale")
+            nc.vector.tensor_tensor(out=scale[:], in0=rstd[:], in1=gain_shift[:, m0 : m0 + tiles], op=ALU.mult)
 
             ys = []
-            for u in range(BANKS):
-                y = work.tile([P, BLOCKS, P], F32, name="y")
-                for j in range(BLOCKS):
-                    m = u * BLOCKS + j
-                    if u % 2 == 0:
+            for s in range(SIDES):
+                y = work.tile([P, blocks * P], F32, name="y")
+                for j in range(blocks):
+                    m = s * blocks + j
+                    shift = gain_shift[:, rows + m0 + m : rows + m0 + m + 1]
+                    if s == 0 or not vector_helps:
                         nc.scalar.activation(
-                            out=y[:, j, :],
-                            in_=zts[u][:, j, :],
+                            out=y[:, j * P : (j + 1) * P],
+                            in_=centred[s][:, j * P : (j + 1) * P],
                             func=ACT.Identity,
-                            bias=bias[:, m : m + 1],
+                            bias=shift,
                             scale=scale[:, m : m + 1],
                         )
                     else:
                         nc.vector.tensor_scalar(
-                            out=y[:, j, :],
-                            in0=zts[u][:, j, :],
+                            out=y[:, j * P : (j + 1) * P],
+                            in0=centred[s][:, j * P : (j + 1) * P],
                             scalar1=scale[:, m : m + 1],
-                            scalar2=bias[:, m : m + 1],
+                            scalar2=shift,
                             op0=ALU.mult,
                             op1=ALU.add,
                         )
                 ys.append(y)
             results = []
-            for u in range(BANKS):
-                r = work.tile([P, BLOCKS, P], F32, name="r")
+            for s in range(SIDES):
+                r = work.tile([P, blocks * P], F32, name="r")
                 nc.vector.scalar_tensor_tensor(
-                    out=r[:], in0=ys[u][:], scalar=NEG_SLOPE, in1=ys[u][:], op0=ALU.mult, op1=ALU.max
+                    out=r[:], in0=ys[s][:], scalar=NEG_SLOPE, in1=ys[s][:], op0=ALU.mult, op1=ALU.max
                 )
                 results.append(r)
             return results
@@ -211,52 +229,63 @@ def tile_yuyipointupdate_pb_k_kernel(tc, h1, w_words, w_scales, g2, b2, out):
         to_store = []
         stored = [0]
 
-        def finish(c, results):
-            for u in range(BANKS):
+        def finish(c, results, vector_helps=True):
+            side_cols = BANK * CHUNK_BANKS[c] // SIDES
+            for s in range(SIDES):
                 rt = psum_rt.tile([P, BANK], F32, name="rt")
-                for j in range(BLOCKS):
-                    nc.tensor.transpose(rt[:, j * P : (j + 1) * P], results[u][:, j, :], ident[:])
-                o0 = c * CHUNK + u * BANK
-                if u % 2 == 0:
-                    nc.scalar.copy(out=o_all[:, o0 : o0 + BANK], in_=rt[:])
+                for j in range(side_cols // P):
+                    nc.tensor.transpose(rt[:, j * P : (j + 1) * P], results[s][:, j * P : (j + 1) * P], ident[:])
+                o0 = first_col[c] + s * side_cols
+                if s == 0 or not vector_helps:
+                    nc.scalar.copy(out=o_all[:, o0 : o0 + side_cols], in_=rt[:, 0:side_cols])
                 else:
-                    nc.vector.tensor_copy(out=o_all[:, o0 : o0 + BANK], in_=rt[:])
-                to_store.append(o0)
+                    nc.vector.tensor_copy(out=o_all[:, o0 : o0 + side_cols], in_=rt[:, 0:side_cols])
+            to_store.append(c)
 
         def store_what_is_ready():
-            for o0 in to_store[stored[0] :]:
-                nc.sync.dma_start(out=out_rows[:, o0 : o0 + BANK], in_=o_all[:, o0 : o0 + BANK])
+            for c in to_store[stored[0] :]:
+                cols = slice(first_col[c], first_col[c] + BANK * CHUNK_BANKS[c])
+                nc.sync.dma_start(out=out_rows[:, cols], in_=o_all[:, cols])
             stored[0] = len(to_store)
 
+        last = chunks - 1
         z_banks = None
-        z_sbs = None
-        results = None
+        results = {}
+        z_sbs = {}
         for i in range(len(pieces)):
             c, g0, n_passes = pieces[i]
+            n_banks = CHUNK_BANKS[c]
             if g0 == 0:
-                z_banks = [psum_z.tile([P, BANK], F32, name="z") for u in range(BANKS)]
+                z_banks = [psum_z.tile([P, BANK], F32, name="z") for u in range(n_banks)]
             if i + AHEAD < len(pieces):
                 load_piece(i + AHEAD)
             else:
                 store_what_is_ready()
             for k in range(n_passes):
                 g = g0 + k
-                for u in range(BANKS):
+                for u in range(n_banks):
+                    col = first_col[c] % PLANE + u * BANK
                     nc.tensor.matmul_mx(
                         out=z_banks[u][:],
                         lhsT=h_codes[:, g, :].bitcast(FP8X4),
                         lhsT_scale=h_scales[:, g, :],
                         rhs=w_tiles[i][:, k, 2 * u * BANK : 2 * (u + 1) * BANK].bitcast(FP4X4),
-                        rhs_scale=planes[c][:, g, u * BANK : (u + 1) * BANK],
+                        rhs_scale=planes[first_col[c] // PLANE][:, g, col : col + BANK],
                         start=(g == 0),
                         stop=(g == PASSES - 1),
                     )
-            if c > 0 and g0 + n_passes == TURN_AT:
-                results = normalise(c - 1, z_sbs)
+            if g0 == 0 and c > 0 and c - 1 != last - 2:
+                results[c - 1] = normalise(c - 1, turn(c - 1, z_sbs[c - 1]), vector_helps=c - 1 < last - 2)
+            if c == last and g0 == BACK_AT:
+                finish(c - 2, results[c - 2], vector_helps=False)
             if g0 + n_passes == PASSES:
-                z_sbs = leave(z_banks)
-                if c > 0:
-                    finish(c - 1, results)
+                z_sbs[c] = leave(c, z_banks, vector_helps=c <= last - 2)
+                if 0 < c < last - 1:
+                    finish(c - 1, results[c - 1])
+                if c == last - 2:
+                    results[c] = normalise(c, turn(c, z_sbs[c]), vector_helps=False)
+        zts = turn(last, z_sbs[last])
+        finish(last - 1, results[last - 1], vector_helps=False)
         store_what_is_ready()
-        finish(CHUNKS - 1, normalise(CHUNKS - 1, z_sbs))
+        finish(last, normalise(last, zts))
         store_what_is_ready()

@@ -101,7 +101,7 @@ def tile_yuyipointupdate_pb_k_kernel(tc, h1, w_words, w_scales, g2, b2, out):
         raws = []
         for b in range(GRAPHS):
             raw = raw_pool.tile([P, PASSES, PACK, NODES], BF16, name="raw")
-            nc.sync.dma_start(
+            (nc.sync if b < GRAPHS // 2 else nc.scalar).dma_start(
                 out=raw[:].rearrange("p g t n -> p g (t n)"),
                 in_=h1[b].rearrange("(g p t) n -> p g (t n)", g=PASSES, p=P, t=PACK),
             )
@@ -165,15 +165,21 @@ def tile_yuyipointupdate_pb_k_kernel(tc, h1, w_words, w_scales, g2, b2, out):
                 zts.append(zt)
             return zts
 
+        def sides_in_order(vector_helps):
+            return (1, 0) if vector_helps else (0, 1)
+
         def normalise(c, zts, vector_helps=True):
             blocks = BANK * CHUNK_BANKS[c] // SIDES // P
             tiles = SIDES * blocks
             stats = small.tile([P, tiles, 6], F32, name="stats")
             mean_var = small.tile([P, tiles, 2], F32, name="mean_var")
-            for m in range(tiles):
-                nc.vector.bn_stats(out=stats[:, m, :], in_=zts[m // blocks][:, (m % blocks) * P : (m % blocks + 1) * P])
-            for m in range(tiles):
-                nc.vector.bn_aggr(out=mean_var[:, m, :], in_=stats[:, m, :])
+            for m in range(tiles + 1):
+                if m < tiles:
+                    nc.vector.bn_stats(
+                        out=stats[:, m, :], in_=zts[m // blocks][:, (m % blocks) * P : (m % blocks + 1) * P]
+                    )
+                if m > 0:
+                    nc.vector.bn_aggr(out=mean_var[:, m - 1, :], in_=stats[:, m - 1, :])
 
             m0 = first_col[c] // P
             std = small.tile([P, tiles], F32, name="std")
@@ -183,14 +189,17 @@ def tile_yuyipointupdate_pb_k_kernel(tc, h1, w_words, w_scales, g2, b2, out):
                 zc = work.tile([P, blocks * P], F32, name="zc")
                 for j in range(blocks):
                     m = s * blocks + j
-                    nc.vector.tensor_scalar_sub(
-                        out=zc[:, j * P : (j + 1) * P], in0=zts[s][:, j * P : (j + 1) * P], scalar1=mean_var[:, m, 0:1]
+                    nc.vector.tensor_scalar(
+                        out=zc[:, j * P : (j + 1) * P],
+                        in0=zts[s][:, j * P : (j + 1) * P],
+                        scalar1=mean_var[:, m, 0:1],
+                        scalar2=gain_shift[:, m0 + m : m0 + m + 1],
+                        op0=ALU.subtract,
+                        op1=ALU.mult,
                     )
                 centred.append(zc)
             rstd = small.tile([P, tiles], F32, name="rstd")
             nc.vector.reciprocal(out=rstd[:], in_=std[:])
-            scale = small.tile([P, tiles], F32, name="scale")
-            nc.vector.tensor_tensor(out=scale[:], in0=rstd[:], in1=gain_shift[:, m0 : m0 + tiles], op=ALU.mult)
 
             ys = []
             for s in range(SIDES):
@@ -204,25 +213,25 @@ def tile_yuyipointupdate_pb_k_kernel(tc, h1, w_words, w_scales, g2, b2, out):
                             in_=centred[s][:, j * P : (j + 1) * P],
                             func=ACT.Identity,
                             bias=shift,
-                            scale=scale[:, m : m + 1],
+                            scale=rstd[:, m : m + 1],
                         )
                     else:
                         nc.vector.tensor_scalar(
                             out=y[:, j * P : (j + 1) * P],
                             in0=centred[s][:, j * P : (j + 1) * P],
-                            scalar1=scale[:, m : m + 1],
+                            scalar1=rstd[:, m : m + 1],
                             scalar2=shift,
                             op0=ALU.mult,
                             op1=ALU.add,
                         )
                 ys.append(y)
-            results = []
-            for s in range(SIDES):
+            results = {}
+            for s in sides_in_order(vector_helps):
                 r = work.tile([P, blocks * P], F32, name="r")
                 nc.vector.scalar_tensor_tensor(
                     out=r[:], in0=ys[s][:], scalar=NEG_SLOPE, in1=ys[s][:], op0=ALU.mult, op1=ALU.max
                 )
-                results.append(r)
+                results[s] = r
             return results
 
         o_all = keep.tile([P, C_OUT], F32)
@@ -231,7 +240,7 @@ def tile_yuyipointupdate_pb_k_kernel(tc, h1, w_words, w_scales, g2, b2, out):
 
         def finish(c, results, vector_helps=True):
             side_cols = BANK * CHUNK_BANKS[c] // SIDES
-            for s in range(SIDES):
+            for s in sides_in_order(vector_helps):
                 rt = psum_rt.tile([P, BANK], F32, name="rt")
                 for j in range(side_cols // P):
                     nc.tensor.transpose(rt[:, j * P : (j + 1) * P], results[s][:, j * P : (j + 1) * P], ident[:])

@@ -19,12 +19,14 @@ C_IN = 8192
 C_OUT = 4096
 PASSES = C_IN // K_PASS
 BANK = 512
-PLANE = 1024
+GROUP_BANKS = (4, 2, 1, 1)
+GROUP_PIECES = ((2, 2, 2, 2, 2, 2, 2, 2), (4, 4, 4, 4), (4, 4, 4, 4), (4, 4, 4, 2, 2))
 CHUNK_BANKS = (2, 2, 2, 1, 1)
-CHUNK_PIECES = ((4, 4, 4, 4), (4, 4, 4, 4), (4, 4, 4, 4), (4, 4, 4, 4), (4, 4, 4, 2, 2))
+GROUP_CHUNKS = ((0, 1), (2,), (3,), (4,))
+PLANE_BANKS = (4, 2, 2)
+GROUP_PLANE = (0, 1, 2, 2)
 SIDES = 2
 AHEAD = 8
-BACK_AT = 8
 SCALE_RUN = 4
 EPS_BN = 1e-5
 NEG_SLOPE = 0.01
@@ -62,12 +64,14 @@ def tile_yuyipointupdate_pb_k_kernel(tc, h1, w_words, w_scales, g2, b2, out):
         planes = {}
 
         def zero_plane(s):
-            plane = keep.tile([P, PASSES, PLANE], U8, name="plane%d" % s, align_bytes=64)
-            nc.vector.memset(plane[:].bitcast(I32), 0)
+            plane = keep.tile([P, PASSES, BANK * PLANE_BANKS[s]], U8, name="plane%d" % s, align_bytes=64)
+            for g0 in range(0, PASSES, SCALE_RUN):
+                nc.vector.memset(plane[:, g0 : g0 + SCALE_RUN, :].bitcast(I32), 0)
             planes[s] = plane
 
         def load_scales(s):
-            cols = slice(s * PLANE // 4, (s + 1) * PLANE // 4)
+            lo = BANK * sum(PLANE_BANKS[:s])
+            cols = slice(lo // 4, (lo + BANK * PLANE_BANKS[s]) // 4)
             for g0 in range(0, PASSES, SCALE_RUN):
                 for r in range(4):
                     nc.sync.dma_start(
@@ -75,23 +79,24 @@ def tile_yuyipointupdate_pb_k_kernel(tc, h1, w_words, w_scales, g2, b2, out):
                         in_=scales_i32[g0 : g0 + SCALE_RUN, r:16:4, cols].rearrange("g q n -> q g n"),
                     )
 
+        group_col = [BANK * sum(GROUP_BANKS[:a]) for a in range(len(GROUP_BANKS))]
         pieces = []
-        for c in range(chunks):
+        for a in range(len(GROUP_BANKS)):
             g0 = 0
-            for n_passes in CHUNK_PIECES[c]:
-                pieces.append((c, g0, n_passes))
+            for n_passes in GROUP_PIECES[a]:
+                pieces.append((a, g0, n_passes))
                 g0 += n_passes
         w_tiles = {}
 
         def load_piece(i):
-            c, g0, n_passes = pieces[i]
-            if g0 == 0 and first_col[c] % PLANE == 0:
-                load_scales(first_col[c] // PLANE)
-            width = BANK * CHUNK_BANKS[c]
+            a, g0, n_passes = pieces[i]
+            if g0 == 0 and (a == 0 or GROUP_PLANE[a] != GROUP_PLANE[a - 1]):
+                load_scales(GROUP_PLANE[a])
+            width = BANK * GROUP_BANKS[a]
             w_tile = w_pool.tile([P, n_passes, 2 * width], U8, name="w_tile", align_bytes=64)
             nc.sync.dma_start(
                 out=w_tile[:].bitcast(I32),
-                in_=words_i32[g0 : g0 + n_passes, :, first_col[c] // 2 : (first_col[c] + width) // 2].rearrange(
+                in_=words_i32[g0 : g0 + n_passes, :, group_col[a] // 2 : (group_col[a] + width) // 2].rearrange(
                     "g p n -> p g n"
                 ),
             )
@@ -106,8 +111,7 @@ def tile_yuyipointupdate_pb_k_kernel(tc, h1, w_words, w_scales, g2, b2, out):
                 in_=h1[b].rearrange("(g p t) n -> p g (t n)", g=PASSES, p=P, t=PACK),
             )
             raws.append(raw)
-        first_loads = len(CHUNK_PIECES[0])
-        for i in range(first_loads):
+        for i in range(AHEAD):
             load_piece(i)
 
         gain_shift_f32 = keep.tile([P, P], F32)
@@ -133,10 +137,8 @@ def tile_yuyipointupdate_pb_k_kernel(tc, h1, w_words, w_scales, g2, b2, out):
                 in_=grouped[:, g0 : g0 + half, :, :].rearrange("p g c t -> p (g c t)"),
             )
 
-        for s in range(1, C_OUT // PLANE):
+        for s in range(1, len(PLANE_BANKS)):
             zero_plane(s)
-        for i in range(first_loads, AHEAD):
-            load_piece(i)
 
         def leave(c, z_banks, vector_helps=True):
             side_cols = BANK * CHUNK_BANKS[c] // SIDES
@@ -152,14 +154,11 @@ def tile_yuyipointupdate_pb_k_kernel(tc, h1, w_words, w_scales, g2, b2, out):
                 z_sbs.append(z_sb)
             return z_sbs
 
-        def turn(c, z_sbs):
+        def turn(c, z_sbs, pool=psum_zt, tag="zt"):
             blocks = BANK * CHUNK_BANKS[c] // SIDES // P
             zts = []
             for z_sb in z_sbs:
-                if c == chunks - 2:
-                    zt = psum_z.tile([P, BANK], F32, name="z")
-                else:
-                    zt = psum_zt.tile([P, BANK], F32, name="zt")
+                zt = pool.tile([P, BANK], F32, name=tag)
                 for j in range(blocks):
                     nc.tensor.transpose(zt[:, j * P : (j + 1) * P], z_sb[:, j * P : (j + 1) * P], ident[:])
                 zts.append(zt)
@@ -168,7 +167,7 @@ def tile_yuyipointupdate_pb_k_kernel(tc, h1, w_words, w_scales, g2, b2, out):
         def sides_in_order(vector_helps):
             return (1, 0) if vector_helps else (0, 1)
 
-        def normalise(c, zts, vector_helps=True):
+        def moments(c, zts):
             blocks = BANK * CHUNK_BANKS[c] // SIDES // P
             tiles = SIDES * blocks
             stats = small.tile([P, tiles, 6], F32, name="stats")
@@ -198,6 +197,12 @@ def tile_yuyipointupdate_pb_k_kernel(tc, h1, w_words, w_scales, g2, b2, out):
                         op1=ALU.mult,
                     )
                 centred.append(zc)
+            return std, centred
+
+        def activate(c, std, centred, vector_helps=True):
+            blocks = BANK * CHUNK_BANKS[c] // SIDES // P
+            tiles = SIDES * blocks
+            m0 = first_col[c] // P
             rstd = small.tile([P, tiles], F32, name="rstd")
             nc.vector.reciprocal(out=rstd[:], in_=std[:])
 
@@ -234,21 +239,36 @@ def tile_yuyipointupdate_pb_k_kernel(tc, h1, w_words, w_scales, g2, b2, out):
                 results[s] = r
             return results
 
+        def normalise(c, zts, vector_helps=True):
+            std, centred = moments(c, zts)
+            return activate(c, std, centred, vector_helps)
+
         o_all = keep.tile([P, C_OUT], F32)
         to_store = []
         stored = [0]
 
-        def finish(c, results, vector_helps=True):
+        def turn_back(c, results, vector_helps=True, pool=psum_rt, tag="rt"):
             side_cols = BANK * CHUNK_BANKS[c] // SIDES
+            rts = {}
             for s in sides_in_order(vector_helps):
-                rt = psum_rt.tile([P, BANK], F32, name="rt")
+                rt = pool.tile([P, BANK], F32, name=tag)
                 for j in range(side_cols // P):
                     nc.tensor.transpose(rt[:, j * P : (j + 1) * P], results[s][:, j * P : (j + 1) * P], ident[:])
-                o0 = first_col[c] + s * side_cols
-                if s == 0 or not vector_helps:
-                    nc.scalar.copy(out=o_all[:, o0 : o0 + side_cols], in_=rt[:, 0:side_cols])
-                else:
-                    nc.vector.tensor_copy(out=o_all[:, o0 : o0 + side_cols], in_=rt[:, 0:side_cols])
+                rts[s] = rt
+            return rts
+
+        def empty(c, rts, s, vector_helps=True):
+            side_cols = BANK * CHUNK_BANKS[c] // SIDES
+            o0 = first_col[c] + s * side_cols
+            if s == 0 or not vector_helps:
+                nc.scalar.copy(out=o_all[:, o0 : o0 + side_cols], in_=rts[s][:, 0:side_cols])
+            else:
+                nc.vector.tensor_copy(out=o_all[:, o0 : o0 + side_cols], in_=rts[s][:, 0:side_cols])
+
+        def finish(c, results, vector_helps=True, pool=psum_rt, tag="rt"):
+            rts = turn_back(c, results, vector_helps, pool, tag)
+            for s in sides_in_order(vector_helps):
+                empty(c, rts, s, vector_helps)
             to_store.append(c)
 
         def store_what_is_ready():
@@ -262,39 +282,55 @@ def tile_yuyipointupdate_pb_k_kernel(tc, h1, w_words, w_scales, g2, b2, out):
         results = {}
         z_sbs = {}
         for i in range(len(pieces)):
-            c, g0, n_passes = pieces[i]
-            n_banks = CHUNK_BANKS[c]
+            a, g0, n_passes = pieces[i]
+            n_banks = GROUP_BANKS[a]
             if g0 == 0:
                 z_banks = [psum_z.tile([P, BANK], F32, name="z") for u in range(n_banks)]
             if i + AHEAD < len(pieces):
                 load_piece(i + AHEAD)
             else:
                 store_what_is_ready()
+            plane = planes[GROUP_PLANE[a]]
+            plane_col = group_col[a] - BANK * sum(PLANE_BANKS[: GROUP_PLANE[a]])
             for k in range(n_passes):
                 g = g0 + k
                 for u in range(n_banks):
-                    col = first_col[c] % PLANE + u * BANK
                     nc.tensor.matmul_mx(
                         out=z_banks[u][:],
                         lhsT=h_codes[:, g, :].bitcast(FP8X4),
                         lhsT_scale=h_scales[:, g, :],
                         rhs=w_tiles[i][:, k, 2 * u * BANK : 2 * (u + 1) * BANK].bitcast(FP4X4),
-                        rhs_scale=planes[first_col[c] // PLANE][:, g, col : col + BANK],
+                        rhs_scale=plane[:, g, plane_col + u * BANK : plane_col + (u + 1) * BANK],
                         start=(g == 0),
                         stop=(g == PASSES - 1),
                     )
-            if g0 == 0 and c > 0 and c - 1 != last - 2:
-                results[c - 1] = normalise(c - 1, turn(c - 1, z_sbs[c - 1]), vector_helps=c - 1 < last - 2)
-            if c == last and g0 == BACK_AT:
-                finish(c - 2, results[c - 2], vector_helps=False)
-            if g0 + n_passes == PASSES:
-                z_sbs[c] = leave(c, z_banks, vector_helps=c <= last - 2)
-                if 0 < c < last - 1:
-                    finish(c - 1, results[c - 1])
-                if c == last - 2:
-                    results[c] = normalise(c, turn(c, z_sbs[c]), vector_helps=False)
+            done = g0 + n_passes
+            if a == 1 and done == PASSES // 2:
+                finish(0, results[0])
+            if a == 3 and g0 == 0:
+                results[3] = normalise(3, turn(3, z_sbs[3], pool=psum_z, tag="z"), vector_helps=False)
+            if done == PASSES:
+                for j, c in enumerate(GROUP_CHUNKS[a]):
+                    z_sbs[c] = leave(c, z_banks[2 * j : 2 * j + CHUNK_BANKS[c]], vector_helps=c <= 2)
+                if a == 0:
+                    zts0 = turn(0, z_sbs[0])
+                    zts1 = turn(1, z_sbs[1], pool=psum_z, tag="z")
+                    results[0] = normalise(0, zts0)
+                    results[1] = normalise(1, zts1)
+                if a == 1:
+                    finish(1, results[1])
+                    results[2] = normalise(2, turn(2, z_sbs[2]), vector_helps=False)
         zts = turn(last, z_sbs[last])
-        finish(last - 1, results[last - 1], vector_helps=False)
+        narrow_rts = turn_back(last - 1, results[last - 1], vector_helps=False)
+        wide_rts = turn_back(last - 2, results[last - 2], vector_helps=False, pool=psum_z, tag="z")
+        empty(last - 1, narrow_rts, 0, vector_helps=False)
+        empty(last - 1, narrow_rts, 1, vector_helps=False)
+        to_store.append(last - 1)
+        std, centred = moments(last, zts)
+        empty(last - 2, wide_rts, 0, vector_helps=False)
+        last_results = activate(last, std, centred)
+        empty(last - 2, wide_rts, 1, vector_helps=False)
+        to_store.append(last - 2)
         store_what_is_ready()
-        finish(last, normalise(last, zts))
+        finish(last, last_results, pool=psum_z, tag="z")
         store_what_is_ready()

@@ -27,7 +27,6 @@ PLANE_BANKS = (4, 2, 2)
 GROUP_PLANE = (0, 1, 2, 2)
 SIDES = 2
 AHEAD = 8
-SCALE_RUN = 4
 EPS_BN = 1e-5
 NEG_SLOPE = 0.01
 
@@ -65,19 +64,19 @@ def tile_yuyipointupdate_pb_k_kernel(tc, h1, w_words, w_scales, g2, b2, out):
 
         def zero_plane(s):
             plane = keep.tile([P, PASSES, BANK * PLANE_BANKS[s]], U8, name="plane%d" % s, align_bytes=64)
-            for g0 in range(0, PASSES, SCALE_RUN):
-                nc.vector.memset(plane[:, g0 : g0 + SCALE_RUN, :].bitcast(I32), 0)
+            nc.vector.memset(plane[:].bitcast(I32), 0)
             planes[s] = plane
 
         def load_scales(s):
             lo = BANK * sum(PLANE_BANKS[:s])
             cols = slice(lo // 4, (lo + BANK * PLANE_BANKS[s]) // 4)
-            for g0 in range(0, PASSES, SCALE_RUN):
-                for r in range(4):
-                    nc.sync.dma_start(
-                        out=planes[s][r:P:32, g0 : g0 + SCALE_RUN, :].bitcast(I32),
-                        in_=scales_i32[g0 : g0 + SCALE_RUN, r:16:4, cols].rearrange("g q n -> q g n"),
-                    )
+            for i in range(16):
+                q = 8 * (i % 2) + i // 2
+                p = 32 * (q // 4) + q % 4
+                nc.sync.dma_start(
+                    out=planes[s][p : p + 1, :, :].bitcast(I32),
+                    in_=scales_i32[:, q : q + 1, cols].rearrange("g q n -> q g n"),
+                )
 
         group_col = [BANK * sum(GROUP_BANKS[:a]) for a in range(len(GROUP_BANKS))]
         pieces = []

@@ -27,6 +27,9 @@ PLANE_BANKS = (4, 2, 2)
 GROUP_PLANE = (0, 1, 2, 2)
 SIDES = 2
 AHEAD = 8
+SCALE_ROWS = 16
+WOVEN = 8
+PAIR = 2
 EPS_BN = 1e-5
 NEG_SLOPE = 0.01
 
@@ -67,10 +70,10 @@ def tile_yuyipointupdate_pb_k_kernel(tc, h1, w_words, w_scales, g2, b2, out):
             nc.vector.memset(plane[:].bitcast(I32), 0)
             planes[s] = plane
 
-        def load_scales(s):
+        def load_scales(s, first, count):
             lo = BANK * sum(PLANE_BANKS[:s])
             cols = slice(lo // 4, (lo + BANK * PLANE_BANKS[s]) // 4)
-            for i in range(16):
+            for i in range(first, first + count):
                 q = 8 * (i % 2) + i // 2
                 p = 32 * (q // 4) + q % 4
                 nc.sync.dma_start(
@@ -80,17 +83,21 @@ def tile_yuyipointupdate_pb_k_kernel(tc, h1, w_words, w_scales, g2, b2, out):
 
         group_col = [BANK * sum(GROUP_BANKS[:a]) for a in range(len(GROUP_BANKS))]
         pieces = []
+        piece_in_group = []
         for a in range(len(GROUP_BANKS)):
             g0 = 0
-            for n_passes in GROUP_PIECES[a]:
+            for j, n_passes in enumerate(GROUP_PIECES[a]):
                 pieces.append((a, g0, n_passes))
+                piece_in_group.append(j)
                 g0 += n_passes
         w_tiles = {}
 
         def load_piece(i):
             a, g0, n_passes = pieces[i]
-            if g0 == 0 and (a == 0 or GROUP_PLANE[a] != GROUP_PLANE[a - 1]):
-                load_scales(GROUP_PLANE[a])
+            if g0 == 0 and a == 0:
+                load_scales(0, 0, SCALE_ROWS)
+            if g0 == 0 and a > 0 and GROUP_PLANE[a] != GROUP_PLANE[a - 1]:
+                load_scales(GROUP_PLANE[a], WOVEN, SCALE_ROWS - WOVEN)
             width = BANK * GROUP_BANKS[a]
             w_tile = w_pool.tile([P, n_passes, 2 * width], U8, name="w_tile", align_bytes=64)
             nc.sync.dma_start(
@@ -100,6 +107,9 @@ def tile_yuyipointupdate_pb_k_kernel(tc, h1, w_words, w_scales, g2, b2, out):
                 ),
             )
             w_tiles[i] = w_tile
+            turn_in_weave = piece_in_group[i] - (len(GROUP_PIECES[a]) - WOVEN // PAIR)
+            if a + 1 < len(GROUP_BANKS) and GROUP_PLANE[a + 1] != GROUP_PLANE[a] and turn_in_weave >= 0:
+                load_scales(GROUP_PLANE[a + 1], PAIR * turn_in_weave, PAIR)
 
         zero_plane(0)
         raws = []
@@ -110,7 +120,8 @@ def tile_yuyipointupdate_pb_k_kernel(tc, h1, w_words, w_scales, g2, b2, out):
                 in_=h1[b].rearrange("(g p t) n -> p g (t n)", g=PASSES, p=P, t=PACK),
             )
             raws.append(raw)
-        for i in range(AHEAD):
+        first_loads = len(GROUP_PIECES[0]) - WOVEN // PAIR
+        for i in range(first_loads):
             load_piece(i)
 
         gain_shift_f32 = keep.tile([P, P], F32)
@@ -138,6 +149,8 @@ def tile_yuyipointupdate_pb_k_kernel(tc, h1, w_words, w_scales, g2, b2, out):
 
         for s in range(1, len(PLANE_BANKS)):
             zero_plane(s)
+        for i in range(first_loads, AHEAD):
+            load_piece(i)
 
         def leave(c, z_banks, vector_helps=True):
             side_cols = BANK * CHUNK_BANKS[c] // SIDES

@@ -193,8 +193,10 @@ def tile_yuyipointupdate_pb_k_kernel(tc, h1, w_words, w_scales, g2, b2, out):
                     nc.vector.bn_aggr(out=mean_var[:, m - 1, :], in_=stats[:, m - 1, :])
 
             m0 = first_col[c] // P
-            std = small.tile([P, tiles], F32, name="std")
-            nc.scalar.activation(out=std[:], in_=mean_var[:, :, 1], func=ACT.Sqrt, bias=eps[:, 0:1], scale=1.0)
+            rstd = small.tile([P, tiles], F32, name="rstd")
+            nc.scalar.activation(
+                out=rstd[:], in_=mean_var[:, :, 1], func=ACT.Abs_reciprocal_sqrt, bias=eps[:, 0:1], scale=1.0
+            )
             centred = []
             for s in range(SIDES):
                 zc = work.tile([P, blocks * P], F32, name="zc")
@@ -209,15 +211,11 @@ def tile_yuyipointupdate_pb_k_kernel(tc, h1, w_words, w_scales, g2, b2, out):
                         op1=ALU.mult,
                     )
                 centred.append(zc)
-            return std, centred
+            return rstd, centred
 
-        def activate(c, std, centred, vector_helps=True):
+        def activate(c, rstd, centred, vector_helps=True):
             blocks = BANK * CHUNK_BANKS[c] // SIDES // P
-            tiles = SIDES * blocks
             m0 = first_col[c] // P
-            rstd = small.tile([P, tiles], F32, name="rstd")
-            nc.vector.reciprocal(out=rstd[:], in_=std[:])
-
             ys = []
             for s in range(SIDES):
                 y = work.tile([P, blocks * P], F32, name="y")
@@ -252,8 +250,8 @@ def tile_yuyipointupdate_pb_k_kernel(tc, h1, w_words, w_scales, g2, b2, out):
             return results
 
         def normalise(c, zts, vector_helps=True):
-            std, centred = moments(c, zts)
-            return activate(c, std, centred, vector_helps)
+            rstd, centred = moments(c, zts)
+            return activate(c, rstd, centred, vector_helps)
 
         o_all = keep.tile([P, C_OUT], F32)
         to_store = []
@@ -338,9 +336,9 @@ def tile_yuyipointupdate_pb_k_kernel(tc, h1, w_words, w_scales, g2, b2, out):
         empty(last - 1, narrow_rts, 0, vector_helps=False)
         empty(last - 1, narrow_rts, 1, vector_helps=False)
         to_store.append(last - 1)
-        std, centred = moments(last, zts)
+        rstd, centred = moments(last, zts)
         empty(last - 2, wide_rts, 0, vector_helps=False)
-        last_results = activate(last, std, centred)
+        last_results = activate(last, rstd, centred)
         empty(last - 2, wide_rts, 1, vector_helps=False)
         to_store.append(last - 2)
         store_what_is_ready()

@@ -15,6 +15,9 @@ P = 128
 PACK = 4
 K_PASS = P * PACK
 GRAPHS, NODES = 4, 32
+PAIRS = GRAPHS // 2
+RUN_WORDS = 16
+VECTOR_PIECES = 10
 C_IN = 8192
 C_OUT = 4096
 PASSES = C_IN // K_PASS
@@ -46,7 +49,7 @@ def tile_yuyipointupdate_pb_k_kernel(tc, h1, w_words, w_scales, g2, b2, out):
     first_col = [BANK * sum(CHUNK_BANKS[:c]) for c in range(chunks)]
 
     with tc.manual_schedule(), tc.tile_pool(name="keep", bufs=1) as keep, tc.tile_pool(
-        name="raw", bufs=GRAPHS
+        name="raw", bufs=GRAPHS // 2
     ) as raw_pool, tc.tile_pool(name="weights", bufs=AHEAD + 1) as w_pool, tc.tile_pool(
         name="work", bufs=2 * SIDES
     ) as work, tc.tile_pool(name="small", bufs=2) as small, tc.psum_pool(
@@ -54,12 +57,15 @@ def tile_yuyipointupdate_pb_k_kernel(tc, h1, w_words, w_scales, g2, b2, out):
     ) as psum_z, tc.psum_pool(name="psum_zt", bufs=SIDES) as psum_zt, tc.psum_pool(
         name="psum_rt", bufs=SIDES
     ) as psum_rt:
+        o_all = keep.tile([P, C_OUT], F32)
         gain_shift_rows = keep.tile([P, P], BF16)
         nc.vector.memset(gain_shift_rows[:], 0.0)
         eps = keep.tile([P, 1], F32)
         nc.vector.memset(eps[:], EPS_BN)
         nc.scalar.dma_start(out=gain_shift_rows[0:rows, :], in_=g2.rearrange("(m p) -> m p", p=P))
         nc.scalar.dma_start(out=gain_shift_rows[rows : 2 * rows, :], in_=b2.rearrange("(m p) -> m p", p=P))
+        zeros = keep.tile([P, BANK], BF16)
+        nc.gpsimd.memset(zeros[:], 0.0)
         ident = keep.tile([P, P], F32)
         make_identity(nc, ident[:])
 
@@ -113,16 +119,106 @@ def tile_yuyipointupdate_pb_k_kernel(tc, h1, w_words, w_scales, g2, b2, out):
 
         zero_plane(0)
         raws = []
-        for b in range(GRAPHS):
-            raw = raw_pool.tile([P, PASSES, PACK, NODES], BF16, name="raw")
-            (nc.sync if b < GRAPHS // 2 else nc.scalar).dma_start(
-                out=raw[:].rearrange("p g t n -> p g (t n)"),
-                in_=h1[b].rearrange("(g p t) n -> p g (t n)", g=PASSES, p=P, t=PACK),
-            )
+        for pair in range(PAIRS):
+            raw = raw_pool.tile([P, 2, RUN_WORDS * PACK * NODES], BF16, name="raw")
+            for i in range(2):
+                (nc.sync if i == 0 else nc.scalar).dma_start(
+                    out=raw[:, i, :], in_=h1[2 * pair + i].rearrange("(s c) n -> s (c n)", s=P)
+                )
             raws.append(raw)
         first_loads = len(GROUP_PIECES[0]) - WOVEN // PAIR
         for i in range(first_loads):
             load_piece(i)
+
+        grouped = keep.tile([P, PASSES, P * PACK // 2], F32, align_bytes=64)
+        h_codes = keep.tile([P, PASSES, P], U32, align_bytes=64)
+        h_scales = keep.tile([P, PASSES, P], U8, align_bytes=64)
+        per_bank = BANK // P
+
+        def copy(engine, out, in_):
+            if engine == 0:
+                nc.scalar.copy(out=out, in_=in_)
+            else:
+                nc.vector.tensor_copy(out=out, in_=in_)
+
+        def quantise(g0, count):
+            nc.vector.quantize_mx(
+                out=h_codes[:, g0 : g0 + count, :].rearrange("p g c -> p (g c)").bitcast(FP8X4),
+                scales=h_scales[:, g0 : g0 + count, :].rearrange("p g c -> p (g c)"),
+                in_=grouped[:, g0 : g0 + count, :].rearrange("p g w -> p (g w)").bitcast(BF16),
+            )
+
+        laid_out = o_all[:].bitcast(BF16).rearrange(
+            "s (a j b n t) -> s a j b n t", a=PAIRS, j=RUN_WORDS, b=2, n=NODES
+        )
+
+        def lay_out(b):
+            src = raws[b // 2][:, b % 2, :].rearrange("s (j t n) -> s j n t", j=RUN_WORDS, t=PACK)
+            for engine, js in ((0, slice(VECTOR_PIECES, RUN_WORDS)), (1, slice(0, VECTOR_PIECES))):
+                copy(engine, laid_out[:, b // 2, js, b % 2, :, :], src[:, js, :, :])
+
+        def turn_pieces(pair):
+            banks = []
+            for k in range(RUN_WORDS // per_bank):
+                bank = psum_z.tile([P, BANK], F32, name="z")
+                for i in range(per_bank):
+                    lo = (pair * RUN_WORDS + per_bank * k + i) * P
+                    nc.tensor.transpose(bank[:, i * P : (i + 1) * P], o_all[:, lo : lo + P], ident[:])
+                banks.append(bank)
+            return banks
+
+        def order_pieces(turned, banks, k):
+            copy(
+                k % 2,
+                turned[:, :, per_bank * k : per_bank * (k + 1)],
+                banks[k][:].rearrange("w (i s) -> w s i", i=per_bank),
+            )
+
+        def bring(pair, turned):
+            turned_cols = turned[:].rearrange("w s j -> w (s j)")
+            last_pair = pair == PAIRS - 1
+            words = 2 * NODES * PACK // 2
+            for k in range(PASSES // per_bank):
+                if k % 2 == 0:
+                    bank = psum_zt.tile([P, BANK], F32, name="zt")
+                else:
+                    bank = psum_rt.tile([P, BANK], F32, name="rt")
+                for i in range(per_bank):
+                    lo = (per_bank * k + i) * P
+                    nc.tensor.transpose(bank[:, i * P : (i + 1) * P], turned_cols[:, lo : lo + P], ident[:])
+                copy(
+                    0 if last_pair else k % 2,
+                    grouped[:, per_bank * k : per_bank * (k + 1), pair * words : (pair + 1) * words],
+                    bank[:].rearrange("p (g w) -> p g w", g=per_bank),
+                )
+                if last_pair:
+                    quantise(per_bank * k, per_bank)
+
+        def keep_warm(count):
+            bank = psum_z.tile([P, BANK], F32, name="z")
+            for i in range(count):
+                nc.tensor.matmul(bank[:], lhsT=zeros[:, 0:P], rhs=zeros[:], start=True, stop=True)
+
+        keep_warm(8)
+        lay_out(0)
+        lay_out(1)
+        lay_out(2)
+        turned_first = raw_pool.tile([P, P, RUN_WORDS], F32, name="raw")
+        banks = turn_pieces(0)
+        order_pieces(turned_first, banks, 0)
+        order_pieces(turned_first, banks, 1)
+        lay_out(3)
+        order_pieces(turned_first, banks, 2)
+        order_pieces(turned_first, banks, 3)
+        keep_warm(2)
+        turned_second = raw_pool.tile([P, P, RUN_WORDS], F32, name="raw")
+        banks = turn_pieces(1)
+        for k in range(len(banks)):
+            order_pieces(turned_second, banks, k)
+        keep_warm(2)
+        bring(0, turned_first)
+        keep_warm(2)
+        bring(1, turned_second)
 
         gain_shift_f32 = keep.tile([P, P], F32)
         nc.scalar.copy(out=gain_shift_f32[:], in_=gain_shift_rows[:])
@@ -130,22 +226,6 @@ def tile_yuyipointupdate_pb_k_kernel(tc, h1, w_words, w_scales, g2, b2, out):
         nc.tensor.transpose(gs_ps[:, 0:P], gain_shift_f32[:], ident[:])
         gain_shift = keep.tile([P, 2 * rows], F32)
         nc.scalar.copy(out=gain_shift[:], in_=gs_ps[:, 0 : 2 * rows])
-
-        grouped = keep.tile([P, PASSES, P, PACK], BF16, align_bytes=64)
-        for b in range(GRAPHS):
-            nc.vector.tensor_copy(
-                out=grouped[:, :, b * NODES : (b + 1) * NODES, :],
-                in_=raws[b][:].rearrange("p g t n -> p g n t"),
-            )
-        h_codes = keep.tile([P, PASSES, P], U32, align_bytes=64)
-        h_scales = keep.tile([P, PASSES, P], U8, align_bytes=64)
-        half = PASSES // 2
-        for g0 in range(0, PASSES, half):
-            nc.vector.quantize_mx(
-                out=h_codes[:, g0 : g0 + half, :].rearrange("p g c -> p (g c)").bitcast(FP8X4),
-                scales=h_scales[:, g0 : g0 + half, :].rearrange("p g c -> p (g c)"),
-                in_=grouped[:, g0 : g0 + half, :, :].rearrange("p g c t -> p (g c t)"),
-            )
 
         for s in range(1, len(PLANE_BANKS)):
             zero_plane(s)
@@ -253,7 +333,6 @@ def tile_yuyipointupdate_pb_k_kernel(tc, h1, w_words, w_scales, g2, b2, out):
             rstd, centred = moments(c, zts)
             return activate(c, rstd, centred, vector_helps)
 
-        o_all = keep.tile([P, C_OUT], F32)
         to_store = []
         stored = [0]
 

@@ -23,7 +23,7 @@ C_OUT = 4096
 PASSES = C_IN // K_PASS
 BANK = 512
 GROUP_BANKS = (4, 2, 1, 1)
-GROUP_PIECES = ((2, 2, 2, 2, 2, 2, 2, 2), (4, 4, 4, 4), (4, 4, 4, 4), (4, 4, 4, 2, 2))
+GROUP_PIECES = ((2, 2, 2, 2, 2, 2, 2, 2), (4, 4, 4, 4), (2, 2, 4, 4, 4), (4, 4, 4, 2, 2))
 CHUNK_BANKS = (2, 2, 2, 1, 1)
 GROUP_CHUNKS = ((0, 1), (2,), (3,), (4,))
 PLANE_BANKS = (4, 2, 2)
@@ -253,7 +253,7 @@ def tile_yuyipointupdate_pb_k_kernel(tc, h1, w_words, w_scales, g2, b2, out):
                 zt = pool.tile([P, BANK], F32, name=tag)
                 for j in range(blocks):
                     nc.tensor.transpose(zt[:, j * P : (j + 1) * P], z_sb[:, j * P : (j + 1) * P], ident[:])
-                zts.append(zt)
+                zts.append([zt[:, j * P : (j + 1) * P] for j in range(blocks)])
             return zts
 
         def sides_in_order(vector_helps):
@@ -266,17 +266,31 @@ def tile_yuyipointupdate_pb_k_kernel(tc, h1, w_words, w_scales, g2, b2, out):
             mean_var = small.tile([P, tiles, 2], F32, name="mean_var")
             for m in range(tiles + 1):
                 if m < tiles:
-                    nc.vector.bn_stats(
-                        out=stats[:, m, :], in_=zts[m // blocks][:, (m % blocks) * P : (m % blocks + 1) * P]
-                    )
+                    nc.vector.bn_stats(out=stats[:, m, :], in_=zts[m // blocks][m % blocks])
                 if m > 0:
                     nc.vector.bn_aggr(out=mean_var[:, m - 1, :], in_=stats[:, m - 1, :])
 
-            m0 = first_col[c] // P
             rstd = small.tile([P, tiles], F32, name="rstd")
             nc.scalar.activation(
                 out=rstd[:], in_=mean_var[:, :, 1], func=ACT.Abs_reciprocal_sqrt, bias=eps[:, 0:1], scale=1.0
             )
+            return mean_var, rstd
+
+        def fold(c, zts, mean_var, rstd):
+            tiles = BANK * CHUNK_BANKS[c] // P
+            m0 = first_col[c] // P
+            scale = small.tile([P, tiles], F32, name="scale")
+            nc.vector.tensor_tensor(out=scale[:], in0=rstd[:], in1=gain_shift[:, m0 : m0 + tiles], op=ALU.mult)
+            product = small.tile([P, tiles], F32, name="product")
+            nc.vector.tensor_tensor(out=product[:], in0=mean_var[:, :, 0], in1=scale[:], op=ALU.mult)
+            bias = small.tile([P, tiles], F32, name="bias")
+            shift = gain_shift[:, rows + m0 : rows + m0 + tiles]
+            nc.vector.tensor_tensor(out=bias[:], in0=shift, in1=product[:], op=ALU.subtract)
+            return zts, scale, bias
+
+        def centre(c, zts, mean_var, rstd):
+            blocks = BANK * CHUNK_BANKS[c] // SIDES // P
+            m0 = first_col[c] // P
             centred = []
             for s in range(SIDES):
                 zc = work.tile([P, blocks * P], F32, name="zc")
@@ -284,38 +298,36 @@ def tile_yuyipointupdate_pb_k_kernel(tc, h1, w_words, w_scales, g2, b2, out):
                     m = s * blocks + j
                     nc.vector.tensor_scalar(
                         out=zc[:, j * P : (j + 1) * P],
-                        in0=zts[s][:, j * P : (j + 1) * P],
+                        in0=zts[s][j],
                         scalar1=mean_var[:, m, 0:1],
                         scalar2=gain_shift[:, m0 + m : m0 + m + 1],
                         op0=ALU.subtract,
                         op1=ALU.mult,
                     )
-                centred.append(zc)
-            return rstd, centred
+                centred.append([zc[:, j * P : (j + 1) * P] for j in range(blocks)])
+            return centred, rstd, gain_shift[:, rows + m0 : rows + m0 + SIDES * blocks]
 
-        def activate(c, rstd, centred, vector_helps=True):
+        def activate(c, values, scale, bias, vector_helps=True):
             blocks = BANK * CHUNK_BANKS[c] // SIDES // P
-            m0 = first_col[c] // P
             ys = []
             for s in range(SIDES):
                 y = work.tile([P, blocks * P], F32, name="y")
                 for j in range(blocks):
                     m = s * blocks + j
-                    shift = gain_shift[:, rows + m0 + m : rows + m0 + m + 1]
                     if s == 0 or not vector_helps:
                         nc.scalar.activation(
                             out=y[:, j * P : (j + 1) * P],
-                            in_=centred[s][:, j * P : (j + 1) * P],
+                            in_=values[s][j],
                             func=ACT.Identity,
-                            bias=shift,
-                            scale=rstd[:, m : m + 1],
+                            bias=bias[:, m : m + 1],
+                            scale=scale[:, m : m + 1],
                         )
                     else:
                         nc.vector.tensor_scalar(
                             out=y[:, j * P : (j + 1) * P],
-                            in0=centred[s][:, j * P : (j + 1) * P],
-                            scalar1=rstd[:, m : m + 1],
-                            scalar2=shift,
+                            in0=values[s][j],
+                            scalar1=scale[:, m : m + 1],
+                            scalar2=bias[:, m : m + 1],
                             op0=ALU.mult,
                             op1=ALU.add,
                         )
@@ -330,8 +342,7 @@ def tile_yuyipointupdate_pb_k_kernel(tc, h1, w_words, w_scales, g2, b2, out):
             return results
 
         def normalise(c, zts, vector_helps=True):
-            rstd, centred = moments(c, zts)
-            return activate(c, rstd, centred, vector_helps)
+            return activate(c, *fold(c, zts, *moments(c, zts)), vector_helps)
 
         to_store = []
         stored = [0]
@@ -353,17 +364,16 @@ def tile_yuyipointupdate_pb_k_kernel(tc, h1, w_words, w_scales, g2, b2, out):
                 nc.scalar.copy(out=o_all[:, o0 : o0 + side_cols], in_=rts[s][:, 0:side_cols])
             else:
                 nc.vector.tensor_copy(out=o_all[:, o0 : o0 + side_cols], in_=rts[s][:, 0:side_cols])
+            to_store.append((o0, o0 + side_cols))
 
         def finish(c, results, vector_helps=True, pool=psum_rt, tag="rt"):
             rts = turn_back(c, results, vector_helps, pool, tag)
             for s in sides_in_order(vector_helps):
                 empty(c, rts, s, vector_helps)
-            to_store.append(c)
 
         def store_what_is_ready():
-            for c in to_store[stored[0] :]:
-                cols = slice(first_col[c], first_col[c] + BANK * CHUNK_BANKS[c])
-                nc.sync.dma_start(out=out_rows[:, cols], in_=o_all[:, cols])
+            for lo, hi in to_store[stored[0] :]:
+                nc.sync.dma_start(out=out_rows[:, lo:hi], in_=o_all[:, lo:hi])
             stored[0] = len(to_store)
 
         last = chunks - 1
@@ -374,31 +384,53 @@ def tile_yuyipointupdate_pb_k_kernel(tc, h1, w_words, w_scales, g2, b2, out):
             a, g0, n_passes = pieces[i]
             n_banks = GROUP_BANKS[a]
             if g0 == 0:
-                z_banks = [psum_z.tile([P, BANK], F32, name="z") for u in range(n_banks)]
+                if a < 2:
+                    z_banks = [psum_z.tile([P, BANK], F32, name="z") for u in range(n_banks)]
+                elif a == 2:
+                    z_banks = [psum_z.tile([P, BANK], F32, name="z") for u in range(BANK // P)]
+                else:
+                    z_banks = [psum_zt.tile([P, BANK], F32, name="zt") for u in range(SIDES)]
+                    z_banks += [psum_rt.tile([P, BANK], F32, name="rt") for u in range(SIDES)]
             if i + AHEAD < len(pieces):
                 load_piece(i + AHEAD)
             else:
                 store_what_is_ready()
             plane = planes[GROUP_PLANE[a]]
             plane_col = group_col[a] - BANK * sum(PLANE_BANKS[: GROUP_PLANE[a]])
-            for k in range(n_passes):
-                g = g0 + k
-                for u in range(n_banks):
-                    nc.tensor.matmul_mx(
-                        out=z_banks[u][:],
-                        lhsT=h_codes[:, g, :].bitcast(FP8X4),
-                        lhsT_scale=h_scales[:, g, :],
-                        rhs=w_tiles[i][:, k, 2 * u * BANK : 2 * (u + 1) * BANK].bitcast(FP4X4),
-                        rhs_scale=plane[:, g, plane_col + u * BANK : plane_col + (u + 1) * BANK],
-                        start=(g == 0),
-                        stop=(g == PASSES - 1),
-                    )
+            if a >= 2:
+                for j in range(BANK // P):
+                    for k in range(n_passes):
+                        g = g0 + k
+                        nc.tensor.matmul_mx(
+                            out=z_banks[j][:, 0:P],
+                            lhsT=w_tiles[i][:, k, 2 * j * P : 2 * (j + 1) * P].bitcast(FP4X4),
+                            lhsT_scale=plane[:, g, plane_col + j * P : plane_col + (j + 1) * P],
+                            rhs=h_codes[:, g, :].bitcast(FP8X4),
+                            rhs_scale=h_scales[:, g, :],
+                            start=(g == 0),
+                            stop=(g == PASSES - 1),
+                        )
+            else:
+                for k in range(n_passes):
+                    g = g0 + k
+                    for u in range(n_banks):
+                        nc.tensor.matmul_mx(
+                            out=z_banks[u][:],
+                            lhsT=h_codes[:, g, :].bitcast(FP8X4),
+                            lhsT_scale=h_scales[:, g, :],
+                            rhs=w_tiles[i][:, k, 2 * u * BANK : 2 * (u + 1) * BANK].bitcast(FP4X4),
+                            rhs_scale=plane[:, g, plane_col + u * BANK : plane_col + (u + 1) * BANK],
+                            start=(g == 0),
+                            stop=(g == PASSES - 1),
+                        )
             done = g0 + n_passes
             if a == 1 and done == PASSES // 2:
                 finish(0, results[0])
-            if a == 3 and g0 == 0:
-                results[3] = normalise(3, turn(3, z_sbs[3], pool=psum_z, tag="z"), vector_helps=False)
-            if done == PASSES:
+            if a == 2 and done == PASSES:
+                results[3] = normalise(
+                    3, [[z_banks[2 * s + j][:, 0:P] for j in range(2)] for s in range(SIDES)], vector_helps=False
+                )
+            if done == PASSES and a < 2:
                 for j, c in enumerate(GROUP_CHUNKS[a]):
                     z_sbs[c] = leave(c, z_banks[2 * j : 2 * j + CHUNK_BANKS[c]], vector_helps=c <= 2)
                 if a == 0:
@@ -409,17 +441,15 @@ def tile_yuyipointupdate_pb_k_kernel(tc, h1, w_words, w_scales, g2, b2, out):
                 if a == 1:
                     finish(1, results[1])
                     results[2] = normalise(2, turn(2, z_sbs[2]), vector_helps=False)
-        zts = turn(last, z_sbs[last])
-        narrow_rts = turn_back(last - 1, results[last - 1], vector_helps=False)
+        zts = [[z_banks[2 * s + j][:, 0:P] for j in range(2)] for s in range(SIDES)]
+        narrow_rts = turn_back(last - 1, results[last - 1], vector_helps=False, pool=psum_z, tag="z")
         wide_rts = turn_back(last - 2, results[last - 2], vector_helps=False, pool=psum_z, tag="z")
         empty(last - 1, narrow_rts, 0, vector_helps=False)
         empty(last - 1, narrow_rts, 1, vector_helps=False)
-        to_store.append(last - 1)
-        rstd, centred = moments(last, zts)
+        centred = centre(last, zts, *moments(last, zts))
+        last_results = activate(last, *centred)
         empty(last - 2, wide_rts, 0, vector_helps=False)
-        last_results = activate(last, rstd, centred)
         empty(last - 2, wide_rts, 1, vector_helps=False)
-        to_store.append(last - 2)
         store_what_is_ready()
         finish(last, last_results, pool=psum_z, tag="z")
         store_what_is_ready()

@@ -31,7 +31,6 @@ GROUP_PLANE = (0, 1, 2, 2)
 SIDES = 2
 AHEAD = 8
 SCALE_ROWS = 16
-WOVEN = 8
 PAIR = 2
 EPS_BN = 1e-5
 NEG_SLOPE = 0.01
@@ -71,10 +70,11 @@ def tile_yuyipointupdate_pb_k_kernel(tc, h1, w_words, w_scales, g2, b2, out):
 
         planes = {}
 
-        def zero_plane(s):
-            plane = keep.tile([P, PASSES, BANK * PLANE_BANKS[s]], U8, name="plane%d" % s, align_bytes=64)
-            nc.vector.memset(plane[:].bitcast(I32), 0)
-            planes[s] = plane
+        for s in range(len(PLANE_BANKS)):
+            planes[s] = keep.tile([P, PASSES, BANK * PLANE_BANKS[s]], U8, name="plane%d" % s, align_bytes=64)
+
+        def zero_passes(s, first, count):
+            nc.vector.memset(planes[s][:, first : first + count, :].bitcast(I32), 0)
 
         def load_scales(s, first, count):
             lo = BANK * sum(PLANE_BANKS[:s])
@@ -100,10 +100,9 @@ def tile_yuyipointupdate_pb_k_kernel(tc, h1, w_words, w_scales, g2, b2, out):
 
         def load_piece(i):
             a, g0, n_passes = pieces[i]
-            if g0 == 0 and a == 0:
-                load_scales(0, 0, SCALE_ROWS)
             if g0 == 0 and a > 0 and GROUP_PLANE[a] != GROUP_PLANE[a - 1]:
-                load_scales(GROUP_PLANE[a], WOVEN, SCALE_ROWS - WOVEN)
+                woven = PAIR * len(GROUP_PIECES[a - 1])
+                load_scales(GROUP_PLANE[a], woven, SCALE_ROWS - woven)
             width = BANK * GROUP_BANKS[a]
             w_tile = w_pool.tile([P, n_passes, 2 * width], U8, name="w_tile", align_bytes=64)
             nc.sync.dma_start(
@@ -113,11 +112,10 @@ def tile_yuyipointupdate_pb_k_kernel(tc, h1, w_words, w_scales, g2, b2, out):
                 ),
             )
             w_tiles[i] = w_tile
-            turn_in_weave = piece_in_group[i] - (len(GROUP_PIECES[a]) - WOVEN // PAIR)
-            if a + 1 < len(GROUP_BANKS) and GROUP_PLANE[a + 1] != GROUP_PLANE[a] and turn_in_weave >= 0:
-                load_scales(GROUP_PLANE[a + 1], PAIR * turn_in_weave, PAIR)
+            if a + 1 < len(GROUP_BANKS) and GROUP_PLANE[a + 1] != GROUP_PLANE[a]:
+                load_scales(GROUP_PLANE[a + 1], PAIR * piece_in_group[i], PAIR)
 
-        zero_plane(0)
+        zero_passes(0, 0, PASSES)
         raws = []
         for pair in range(PAIRS):
             raw = raw_pool.tile([P, 2, RUN_WORDS * PACK * NODES], BF16, name="raw")
@@ -126,9 +124,7 @@ def tile_yuyipointupdate_pb_k_kernel(tc, h1, w_words, w_scales, g2, b2, out):
                     out=raw[:, i, :], in_=h1[2 * pair + i].rearrange("(s c) n -> s (c n)", s=P)
                 )
             raws.append(raw)
-        first_loads = len(GROUP_PIECES[0]) - WOVEN // PAIR
-        for i in range(first_loads):
-            load_piece(i)
+        load_scales(0, 0, SCALE_ROWS)
 
         grouped = keep.tile([P, PASSES, P * PACK // 2], F32, align_bytes=64)
         h_codes = keep.tile([P, PASSES, P], U32, align_bytes=64)
@@ -210,13 +206,16 @@ def tile_yuyipointupdate_pb_k_kernel(tc, h1, w_words, w_scales, g2, b2, out):
         lay_out(3)
         order_pieces(turned_first, banks, 2)
         order_pieces(turned_first, banks, 3)
+        zero_passes(1, 0, 4)
         keep_warm(2)
         turned_second = raw_pool.tile([P, P, RUN_WORDS], F32, name="raw")
         banks = turn_pieces(1)
         for k in range(len(banks)):
             order_pieces(turned_second, banks, k)
+        zero_passes(1, 4, 6)
         keep_warm(2)
         bring(0, turned_first)
+        zero_passes(1, 10, 6)
         keep_warm(2)
         bring(1, turned_second)
 
@@ -227,9 +226,8 @@ def tile_yuyipointupdate_pb_k_kernel(tc, h1, w_words, w_scales, g2, b2, out):
         gain_shift = keep.tile([P, 2 * rows], F32)
         nc.scalar.copy(out=gain_shift[:], in_=gs_ps[:, 0 : 2 * rows])
 
-        for s in range(1, len(PLANE_BANKS)):
-            zero_plane(s)
-        for i in range(first_loads, AHEAD):
+        zero_passes(2, 0, PASSES)
+        for i in range(AHEAD):
             load_piece(i)
 
         def leave(c, z_banks, vector_helps=True):

@@ -23,7 +23,7 @@ C_OUT = 4096
 PASSES = C_IN // K_PASS
 BANK = 512
 GROUP_BANKS = (4, 2, 1, 1)
-GROUP_PIECES = ((2, 2, 2, 2, 2, 2, 2, 2), (4, 4, 4, 4), (2, 2, 4, 4, 4), (4, 4, 4, 2, 2))
+GROUP_PIECES = ((2, 2, 2, 2, 2, 2, 2, 2), (2, 2, 2, 2, 2, 2, 2, 2), (2, 2, 4, 4, 4), (4, 4, 4, 2, 2))
 CHUNK_BANKS = (2, 2, 2, 1, 1)
 GROUP_CHUNKS = ((0, 1), (2,), (3,), (4,))
 PLANE_BANKS = (4, 2, 2)
@@ -153,78 +153,78 @@ def tile_yuyipointupdate_pb_k_kernel(tc, h1, w_words, w_scales, g2, b2, out):
             for engine, js in ((0, slice(VECTOR_PIECES, RUN_WORDS)), (1, slice(0, VECTOR_PIECES))):
                 copy(engine, laid_out[:, b // 2, js, b % 2, :, :], src[:, js, :, :])
 
-        def turn_pieces(pair):
+        def bank_for(pair, k):
+            if pair == 0:
+                return psum_z.tile([P, BANK], F32, name="z")
+            if k % 2 == 0:
+                return psum_zt.tile([P, BANK], F32, name="zt")
+            return psum_rt.tile([P, BANK], F32, name="rt")
+
+        def keep_warm(count, bank):
+            for i in range(count):
+                nc.tensor.matmul(bank[:], lhsT=zeros[:, 0:P], rhs=zeros[:], start=True, stop=True)
+
+        def turn_pieces(pair, warm):
             banks = []
             for k in range(RUN_WORDS // per_bank):
-                bank = psum_z.tile([P, BANK], F32, name="z")
+                bank = bank_for(pair, k)
+                if k == 0:
+                    keep_warm(warm, bank)
                 for i in range(per_bank):
                     lo = (pair * RUN_WORDS + per_bank * k + i) * P
                     nc.tensor.transpose(bank[:, i * P : (i + 1) * P], o_all[:, lo : lo + P], ident[:])
                 banks.append(bank)
             return banks
 
-        def order_pieces(turned, banks, k):
-            copy(
-                k % 2,
-                turned[:, :, per_bank * k : per_bank * (k + 1)],
-                banks[k][:].rearrange("w (i s) -> w s i", i=per_bank),
-            )
+        def order_pieces(turned, banks):
+            for k, bank in enumerate(banks):
+                copy(
+                    k % 2,
+                    turned[:, :, per_bank * k : per_bank * (k + 1)],
+                    bank[:].rearrange("w (i s) -> w s i", i=per_bank),
+                )
 
-        def bring(pair, turned):
+        def bring(pair, turned, warm):
             turned_cols = turned[:].rearrange("w s j -> w (s j)")
-            last_pair = pair == PAIRS - 1
             words = 2 * NODES * PACK // 2
             for k in range(PASSES // per_bank):
-                if k % 2 == 0:
-                    bank = psum_zt.tile([P, BANK], F32, name="zt")
-                else:
-                    bank = psum_rt.tile([P, BANK], F32, name="rt")
+                bank = bank_for(pair, k)
+                if k == 0:
+                    keep_warm(warm, bank)
                 for i in range(per_bank):
                     lo = (per_bank * k + i) * P
                     nc.tensor.transpose(bank[:, i * P : (i + 1) * P], turned_cols[:, lo : lo + P], ident[:])
-                copy(
-                    0 if last_pair else k % 2,
-                    grouped[:, per_bank * k : per_bank * (k + 1), pair * words : (pair + 1) * words],
-                    bank[:].rearrange("p (g w) -> p g w", g=per_bank),
-                )
-                if last_pair:
-                    quantise(per_bank * k, per_bank)
+                brought = bank[:].rearrange("p (g w) -> p g w", g=per_bank)
+                if pair == 0:
+                    copy(k % 2, grouped[:, per_bank * k : per_bank * (k + 1), 0:words], brought)
+                    continue
+                step = per_bank // 2 if k == 0 else per_bank
+                for g in range(0, per_bank, step):
+                    g0 = per_bank * k + g
+                    copy(0, grouped[:, g0 : g0 + step, words : 2 * words], brought[:, g : g + step, :])
+                    quantise(g0, step)
 
-        def keep_warm(count):
-            bank = psum_z.tile([P, BANK], F32, name="z")
-            for i in range(count):
-                nc.tensor.matmul(bank[:], lhsT=zeros[:, 0:P], rhs=zeros[:], start=True, stop=True)
-
-        keep_warm(8)
         lay_out(0)
         lay_out(1)
         lay_out(2)
-        turned_first = raw_pool.tile([P, P, RUN_WORDS], F32, name="raw")
-        banks = turn_pieces(0)
-        order_pieces(turned_first, banks, 0)
-        order_pieces(turned_first, banks, 1)
         lay_out(3)
-        order_pieces(turned_first, banks, 2)
-        order_pieces(turned_first, banks, 3)
-        zero_passes(1, 0, 4)
-        keep_warm(2)
+        turned_first = raw_pool.tile([P, P, RUN_WORDS], F32, name="raw")
+        order_pieces(turned_first, turn_pieces(0, warm=18))
+        zero_passes(1, 0, PASSES // 2)
         turned_second = raw_pool.tile([P, P, RUN_WORDS], F32, name="raw")
-        banks = turn_pieces(1)
-        for k in range(len(banks)):
-            order_pieces(turned_second, banks, k)
-        zero_passes(1, 4, 6)
-        keep_warm(2)
-        bring(0, turned_first)
-        zero_passes(1, 10, 6)
-        keep_warm(2)
-        bring(1, turned_second)
+        order_pieces(turned_second, turn_pieces(1, warm=2))
+        zero_passes(1, PASSES // 2, PASSES // 2)
+        bring(0, turned_first, warm=2)
+        bring(1, turned_second, warm=2)
 
         gain_shift_f32 = keep.tile([P, P], F32)
-        nc.scalar.copy(out=gain_shift_f32[:], in_=gain_shift_rows[:])
-        gs_ps = psum_zt.tile([P, BANK], F32, name="zt")
-        nc.tensor.transpose(gs_ps[:, 0:P], gain_shift_f32[:], ident[:])
         gain_shift = keep.tile([P, 2 * rows], F32)
-        nc.scalar.copy(out=gain_shift[:], in_=gs_ps[:, 0 : 2 * rows])
+
+        def turn_gain_shift():
+            nc.scalar.copy(out=gain_shift_f32[:], in_=gain_shift_rows[:])
+            gs_ps = psum_zt.tile([P, BANK], F32, name="zt")
+            nc.tensor.transpose(gs_ps[:, 0:P], gain_shift_f32[:], ident[:])
+            nc.scalar.copy(out=gain_shift[:], in_=gs_ps[:, 0 : 2 * rows])
 
         zero_passes(2, 0, PASSES)
         for i in range(AHEAD):
@@ -422,6 +422,8 @@ def tile_yuyipointupdate_pb_k_kernel(tc, h1, w_words, w_scales, g2, b2, out):
                             stop=(g == PASSES - 1),
                         )
             done = g0 + n_passes
+            if a == 0 and g0 == 0:
+                turn_gain_shift()
             if a == 1 and done == PASSES // 2:
                 finish(0, results[0])
             if a == 2 and done == PASSES:

import concourse.mybir as mybir
from concourse.masks import make_identity

F32 = mybir.dt.float32
BF16 = mybir.dt.bfloat16
I32 = mybir.dt.int32
U32 = mybir.dt.uint32
U8 = mybir.dt.uint8
FP8X4 = mybir.dt.float8_e4m3fn_x4
FP4X4 = mybir.dt.float4_e2m1fn_x4
ALU = mybir.AluOpType
ACT = mybir.ActivationFunctionType

P = 128
PACK = 4
K_PASS = P * PACK
GRAPHS, NODES = 4, 32
PAIRS = GRAPHS // 2
RUN_WORDS = 16
VECTOR_PIECES = 10
C_IN = 8192
C_OUT = 4096
PASSES = C_IN // K_PASS
BANK = 512
GROUP_BANKS = (4, 2, 1, 1)
GROUP_PIECES = ((2, 2, 2, 2, 2, 2, 2, 2), (2, 2, 2, 2, 2, 2, 2, 2), (2, 2, 4, 4, 4), (4, 4, 4, 2, 2))
CHUNK_BANKS = (2, 2, 2, 1, 1)
GROUP_CHUNKS = ((0, 1), (2,), (3,), (4,))
PLANE_BANKS = (4, 2, 2)
GROUP_PLANE = (0, 1, 2, 2)
SIDES = 2
AHEAD = 8
SCALE_ROWS = 16
PAIR = 2
EPS_BN = 1e-5
NEG_SLOPE = 0.01

FLOPS = 2 * GRAPHS * NODES * C_OUT * C_IN


def tile_yuyipointupdate_pb_k_kernel(tc, h1, w_words, w_scales, g2, b2, out):
    nc = tc.nc
    words_i32 = w_words.bitcast(I32)
    scales_i32 = w_scales.bitcast(I32)
    out_rows = out.rearrange("b n o -> (b n) o")
    rows = C_OUT // P
    chunks = len(CHUNK_BANKS)
    first_col = [BANK * sum(CHUNK_BANKS[:c]) for c in range(chunks)]

    with tc.manual_schedule(), tc.tile_pool(name="keep", bufs=1) as keep, tc.tile_pool(
        name="raw", bufs=GRAPHS // 2
    ) as raw_pool, tc.tile_pool(name="weights", bufs=AHEAD + 1) as w_pool, tc.tile_pool(
        name="work", bufs=2 * SIDES
    ) as work, tc.tile_pool(name="small", bufs=2) as small, tc.psum_pool(
        name="psum_z", bufs=4
    ) as psum_z, tc.psum_pool(name="psum_zt", bufs=SIDES) as psum_zt, tc.psum_pool(
        name="psum_rt", bufs=SIDES
    ) as psum_rt:
        o_all = keep.tile([P, C_OUT], F32)
        gain_shift_rows = keep.tile([P, P], BF16)
        nc.vector.memset(gain_shift_rows[:], 0.0)
        eps = keep.tile([P, 1], F32)
        nc.vector.memset(eps[:], EPS_BN)
        nc.scalar.dma_start(out=gain_shift_rows[0:rows, :], in_=g2.rearrange("(m p) -> m p", p=P))
        nc.scalar.dma_start(out=gain_shift_rows[rows : 2 * rows, :], in_=b2.rearrange("(m p) -> m p", p=P))
        zeros = keep.tile([P, BANK], BF16)
        nc.gpsimd.memset(zeros[:], 0.0)
        ident = keep.tile([P, P], F32)
        make_identity(nc, ident[:])

        planes = {}

        for s in range(len(PLANE_BANKS)):
            planes[s] = keep.tile([P, PASSES, BANK * PLANE_BANKS[s]], U8, name="plane%d" % s, align_bytes=64)

        def zero_passes(s, first, count):
            nc.vector.memset(planes[s][:, first : first + count, :].bitcast(I32), 0)

        def load_scales(s, first, count):
            lo = BANK * sum(PLANE_BANKS[:s])
            cols = slice(lo // 4, (lo + BANK * PLANE_BANKS[s]) // 4)
            for i in range(first, first + count):
                q = 8 * (i % 2) + i // 2
                p = 32 * (q // 4) + q % 4
                nc.sync.dma_start(
                    out=planes[s][p : p + 1, :, :].bitcast(I32),
                    in_=scales_i32[:, q : q + 1, cols].rearrange("g q n -> q g n"),
                )

        group_col = [BANK * sum(GROUP_BANKS[:a]) for a in range(len(GROUP_BANKS))]
        pieces = []
        piece_in_group = []
        for a in range(len(GROUP_BANKS)):
            g0 = 0
            for j, n_passes in enumerate(GROUP_PIECES[a]):
                pieces.append((a, g0, n_passes))
                piece_in_group.append(j)
                g0 += n_passes
        w_tiles = {}

        def load_piece(i):
            a, g0, n_passes = pieces[i]
            if g0 == 0 and a > 0 and GROUP_PLANE[a] != GROUP_PLANE[a - 1]:
                woven = PAIR * len(GROUP_PIECES[a - 1])
                load_scales(GROUP_PLANE[a], woven, SCALE_ROWS - woven)
            width = BANK * GROUP_BANKS[a]
            w_tile = w_pool.tile([P, n_passes, 2 * width], U8, name="w_tile", align_bytes=64)
            nc.sync.dma_start(
                out=w_tile[:].bitcast(I32),
                in_=words_i32[g0 : g0 + n_passes, :, group_col[a] // 2 : (group_col[a] + width) // 2].rearrange(
                    "g p n -> p g n"
                ),
            )
            w_tiles[i] = w_tile
            if a + 1 < len(GROUP_BANKS) and GROUP_PLANE[a + 1] != GROUP_PLANE[a]:
                load_scales(GROUP_PLANE[a + 1], PAIR * piece_in_group[i], PAIR)

        zero_passes(0, 0, PASSES)
        raws = []
        for pair in range(PAIRS):
            raw = raw_pool.tile([P, 2, RUN_WORDS * PACK * NODES], BF16, name="raw")
            for i in range(2):
                (nc.sync if i == 0 else nc.scalar).dma_start(
                    out=raw[:, i, :], in_=h1[2 * pair + i].rearrange("(s c) n -> s (c n)", s=P)
                )
            raws.append(raw)
        load_scales(0, 0, SCALE_ROWS)

        grouped = keep.tile([P, PASSES, P * PACK // 2], F32, align_bytes=64)
        h_codes = keep.tile([P, PASSES, P], U32, align_bytes=64)
        h_scales = keep.tile([P, PASSES, P], U8, align_bytes=64)
        per_bank = BANK // P

        def copy(engine, out, in_):
            if engine == 0:
                nc.scalar.copy(out=out, in_=in_)
            else:
                nc.vector.tensor_copy(out=out, in_=in_)

        def quantise(g0, count):
            nc.vector.quantize_mx(
                out=h_codes[:, g0 : g0 + count, :].rearrange("p g c -> p (g c)").bitcast(FP8X4),
                scales=h_scales[:, g0 : g0 + count, :].rearrange("p g c -> p (g c)"),
                in_=grouped[:, g0 : g0 + count, :].rearrange("p g w -> p (g w)").bitcast(BF16),
            )

        laid_out = o_all[:].bitcast(BF16).rearrange(
            "s (a j b n t) -> s a j b n t", a=PAIRS, j=RUN_WORDS, b=2, n=NODES
        )

        def lay_out(b):
            src = raws[b // 2][:, b % 2, :].rearrange("s (j t n) -> s j n t", j=RUN_WORDS, t=PACK)
            for engine, js in ((0, slice(VECTOR_PIECES, RUN_WORDS)), (1, slice(0, VECTOR_PIECES))):
                copy(engine, laid_out[:, b // 2, js, b % 2, :, :], src[:, js, :, :])

        def bank_for(pair, k):
            if pair == 0:
                return psum_z.tile([P, BANK], F32, name="z")
            if k % 2 == 0:
                return psum_zt.tile([P, BANK], F32, name="zt")
            return psum_rt.tile([P, BANK], F32, name="rt")

        def keep_warm(count, bank):
            for i in range(count):
                nc.tensor.matmul(bank[:], lhsT=zeros[:, 0:P], rhs=zeros[:], start=True, stop=True)

        def turn_pieces(pair, warm):
            banks = []
            for k in range(RUN_WORDS // per_bank):
                bank = bank_for(pair, k)
                if k == 0:
                    keep_warm(warm, bank)
                for i in range(per_bank):
                    lo = (pair * RUN_WORDS + per_bank * k + i) * P
                    nc.tensor.transpose(bank[:, i * P : (i + 1) * P], o_all[:, lo : lo + P], ident[:])
                banks.append(bank)
            return banks

        def order_pieces(turned, banks):
            for k, bank in enumerate(banks):
                copy(
                    k % 2,
                    turned[:, :, per_bank * k : per_bank * (k + 1)],
                    bank[:].rearrange("w (i s) -> w s i", i=per_bank),
                )

        def bring(pair, turned, warm):
            turned_cols = turned[:].rearrange("w s j -> w (s j)")
            words = 2 * NODES * PACK // 2
            for k in range(PASSES // per_bank):
                bank = bank_for(pair, k)
                if k == 0:
                    keep_warm(warm, bank)
                for i in range(per_bank):
                    lo = (per_bank * k + i) * P
                    nc.tensor.transpose(bank[:, i * P : (i + 1) * P], turned_cols[:, lo : lo + P], ident[:])
                brought = bank[:].rearrange("p (g w) -> p g w", g=per_bank)
                if pair == 0:
                    copy(k % 2, grouped[:, per_bank * k : per_bank * (k + 1), 0:words], brought)
                    continue
                step = per_bank // 2 if k == 0 else per_bank
                for g in range(0, per_bank, step):
                    g0 = per_bank * k + g
                    copy(0, grouped[:, g0 : g0 + step, words : 2 * words], brought[:, g : g + step, :])
                    quantise(g0, step)

        lay_out(0)
        lay_out(1)
        lay_out(2)
        lay_out(3)
        turned_first = raw_pool.tile([P, P, RUN_WORDS], F32, name="raw")
        order_pieces(turned_first, turn_pieces(0, warm=18))
        zero_passes(1, 0, PASSES // 2)
        turned_second = raw_pool.tile([P, P, RUN_WORDS], F32, name="raw")
        order_pieces(turned_second, turn_pieces(1, warm=2))
        zero_passes(1, PASSES // 2, PASSES // 2)
        bring(0, turned_first, warm=2)
        bring(1, turned_second, warm=2)

        gain_shift_f32 = keep.tile([P, P], F32)
        gain_shift = keep.tile([P, 2 * rows], F32)

        def turn_gain_shift():
            nc.scalar.copy(out=gain_shift_f32[:], in_=gain_shift_rows[:])
            gs_ps = psum_zt.tile([P, BANK], F32, name="zt")
            nc.tensor.transpose(gs_ps[:, 0:P], gain_shift_f32[:], ident[:])
            nc.scalar.copy(out=gain_shift[:], in_=gs_ps[:, 0 : 2 * rows])

        zero_passes(2, 0, PASSES)
        for i in range(AHEAD):
            load_piece(i)

        def leave(c, z_banks, vector_helps=True):
            side_cols = BANK * CHUNK_BANKS[c] // SIDES
            z_sbs = []
            for s in range(SIDES):
                z_sb = work.tile([P, side_cols], F32, name="z_sb")
                src_bank = z_banks[s * side_cols // BANK]
                lo = s * side_cols % BANK
                if s == 0 or len(z_banks) == 1 or not vector_helps:
                    nc.scalar.copy(out=z_sb[:], in_=src_bank[:, lo : lo + side_cols])
                else:
                    nc.vector.tensor_copy(out=z_sb[:], in_=src_bank[:, lo : lo + side_cols])
                z_sbs.append(z_sb)
            return z_sbs

        def turn(c, z_sbs, pool=psum_zt, tag="zt"):
            blocks = BANK * CHUNK_BANKS[c] // SIDES // P
            zts = []
            for z_sb in z_sbs:
                zt = pool.tile([P, BANK], F32, name=tag)
                for j in range(blocks):
                    nc.tensor.transpose(zt[:, j * P : (j + 1) * P], z_sb[:, j * P : (j + 1) * P], ident[:])
                zts.append([zt[:, j * P : (j + 1) * P] for j in range(blocks)])
            return zts

        def sides_in_order(vector_helps):
            return (1, 0) if vector_helps else (0, 1)

        def moments(c, zts):
            blocks = BANK * CHUNK_BANKS[c] // SIDES // P
            tiles = SIDES * blocks
            stats = small.tile([P, tiles, 6], F32, name="stats")
            mean_var = small.tile([P, tiles, 2], F32, name="mean_var")
            for m in range(tiles + 1):
                if m < tiles:
                    nc.vector.bn_stats(out=stats[:, m, :], in_=zts[m // blocks][m % blocks])
                if m > 0:
                    nc.vector.bn_aggr(out=mean_var[:, m - 1, :], in_=stats[:, m - 1, :])

            rstd = small.tile([P, tiles], F32, name="rstd")
            nc.scalar.activation(
                out=rstd[:], in_=mean_var[:, :, 1], func=ACT.Abs_reciprocal_sqrt, bias=eps[:, 0:1], scale=1.0
            )
            return mean_var, rstd

        def fold(c, zts, mean_var, rstd):
            tiles = BANK * CHUNK_BANKS[c] // P
            m0 = first_col[c] // P
            scale = small.tile([P, tiles], F32, name="scale")
            nc.vector.tensor_tensor(out=scale[:], in0=rstd[:], in1=gain_shift[:, m0 : m0 + tiles], op=ALU.mult)
            product = small.tile([P, tiles], F32, name="product")
            nc.vector.tensor_tensor(out=product[:], in0=mean_var[:, :, 0], in1=scale[:], op=ALU.mult)
            bias = small.tile([P, tiles], F32, name="bias")
            shift = gain_shift[:, rows + m0 : rows + m0 + tiles]
            nc.vector.tensor_tensor(out=bias[:], in0=shift, in1=product[:], op=ALU.subtract)
            return zts, scale, bias

        def centre(c, zts, mean_var, rstd):
            blocks = BANK * CHUNK_BANKS[c] // SIDES // P
            m0 = first_col[c] // P
            centred = []
            for s in range(SIDES):
                zc = work.tile([P, blocks * P], F32, name="zc")
                for j in range(blocks):
                    m = s * blocks + j
                    nc.vector.tensor_scalar(
                        out=zc[:, j * P : (j + 1) * P],
                        in0=zts[s][j],
                        scalar1=mean_var[:, m, 0:1],
                        scalar2=gain_shift[:, m0 + m : m0 + m + 1],
                        op0=ALU.subtract,
                        op1=ALU.mult,
                    )
                centred.append([zc[:, j * P : (j + 1) * P] for j in range(blocks)])
            return centred, rstd, gain_shift[:, rows + m0 : rows + m0 + SIDES * blocks]

        def activate(c, values, scale, bias, vector_helps=True):
            blocks = BANK * CHUNK_BANKS[c] // SIDES // P
            ys = []
            for s in range(SIDES):
                y = work.tile([P, blocks * P], F32, name="y")
                for j in range(blocks):
                    m = s * blocks + j
                    if s == 0 or not vector_helps:
                        nc.scalar.activation(
                            out=y[:, j * P : (j + 1) * P],
                            in_=values[s][j],
                            func=ACT.Identity,
                            bias=bias[:, m : m + 1],
                            scale=scale[:, m : m + 1],
                        )
                    else:
                        nc.vector.tensor_scalar(
                            out=y[:, j * P : (j + 1) * P],
                            in0=values[s][j],
                            scalar1=scale[:, m : m + 1],
                            scalar2=bias[:, m : m + 1],
                            op0=ALU.mult,
                            op1=ALU.add,
                        )
                ys.append(y)
            results = {}
            for s in sides_in_order(vector_helps):
                r = work.tile([P, blocks * P], F32, name="r")
                nc.vector.scalar_tensor_tensor(
                    out=r[:], in0=ys[s][:], scalar=NEG_SLOPE, in1=ys[s][:], op0=ALU.mult, op1=ALU.max
                )
                results[s] = r
            return results

        def normalise(c, zts, vector_helps=True):
            return activate(c, *fold(c, zts, *moments(c, zts)), vector_helps)

        to_store = []
        stored = [0]

        def turn_back(c, results, vector_helps=True, pool=psum_rt, tag="rt"):
            side_cols = BANK * CHUNK_BANKS[c] // SIDES
            rts = {}
            for s in sides_in_order(vector_helps):
                rt = pool.tile([P, BANK], F32, name=tag)
                for j in range(side_cols // P):
                    nc.tensor.transpose(rt[:, j * P : (j + 1) * P], results[s][:, j * P : (j + 1) * P], ident[:])
                rts[s] = rt
            return rts

        def empty(c, rts, s, vector_helps=True):
            side_cols = BANK * CHUNK_BANKS[c] // SIDES
            o0 = first_col[c] + s * side_cols
            if s == 0 or not vector_helps:
                nc.scalar.copy(out=o_all[:, o0 : o0 + side_cols], in_=rts[s][:, 0:side_cols])
            else:
                nc.vector.tensor_copy(out=o_all[:, o0 : o0 + side_cols], in_=rts[s][:, 0:side_cols])
            to_store.append((o0, o0 + side_cols))

        def finish(c, results, vector_helps=True, pool=psum_rt, tag="rt"):
            rts = turn_back(c, results, vector_helps, pool, tag)
            for s in sides_in_order(vector_helps):
                empty(c, rts, s, vector_helps)

        def store_what_is_ready():
            for lo, hi in to_store[stored[0] :]:
                nc.sync.dma_start(out=out_rows[:, lo:hi], in_=o_all[:, lo:hi])
            stored[0] = len(to_store)

        last = chunks - 1
        z_banks = None
        results = {}
        z_sbs = {}
        for i in range(len(pieces)):
            a, g0, n_passes = pieces[i]
            n_banks = GROUP_BANKS[a]
            if g0 == 0:
                if a < 2:
                    z_banks = [psum_z.tile([P, BANK], F32, name="z") for u in range(n_banks)]
                elif a == 2:
                    z_banks = [psum_z.tile([P, BANK], F32, name="z") for u in range(BANK // P)]
                else:
                    z_banks = [psum_zt.tile([P, BANK], F32, name="zt") for u in range(SIDES)]
                    z_banks += [psum_rt.tile([P, BANK], F32, name="rt") for u in range(SIDES)]
            if i + AHEAD < len(pieces):
                load_piece(i + AHEAD)
            else:
                store_what_is_ready()
            plane = planes[GROUP_PLANE[a]]
            plane_col = group_col[a] - BANK * sum(PLANE_BANKS[: GROUP_PLANE[a]])
            if a >= 2:
                for j in range(BANK // P):
                    for k in range(n_passes):
                        g = g0 + k
                        nc.tensor.matmul_mx(
                            out=z_banks[j][:, 0:P],
                            lhsT=w_tiles[i][:, k, 2 * j * P : 2 * (j + 1) * P].bitcast(FP4X4),
                            lhsT_scale=plane[:, g, plane_col + j * P : plane_col + (j + 1) * P],
                            rhs=h_codes[:, g, :].bitcast(FP8X4),
                            rhs_scale=h_scales[:, g, :],
                            start=(g == 0),
                            stop=(g == PASSES - 1),
                        )
            else:
                for k in range(n_passes):
                    g = g0 + k
                    for u in range(n_banks):
                        nc.tensor.matmul_mx(
                            out=z_banks[u][:],
                            lhsT=h_codes[:, g, :].bitcast(FP8X4),
                            lhsT_scale=h_scales[:, g, :],
                            rhs=w_tiles[i][:, k, 2 * u * BANK : 2 * (u + 1) * BANK].bitcast(FP4X4),
                            rhs_scale=plane[:, g, plane_col + u * BANK : plane_col + (u + 1) * BANK],
                            start=(g == 0),
                            stop=(g == PASSES - 1),
                        )
            done = g0 + n_passes
            if a == 0 and g0 == 0:
                turn_gain_shift()
            if a == 1 and done == PASSES // 2:
                finish(0, results[0])
            if a == 2 and done == PASSES:
                results[3] = normalise(
                    3, [[z_banks[2 * s + j][:, 0:P] for j in range(2)] for s in range(SIDES)], vector_helps=False
                )
            if done == PASSES and a < 2:
                for j, c in enumerate(GROUP_CHUNKS[a]):
                    z_sbs[c] = leave(c, z_banks[2 * j : 2 * j + CHUNK_BANKS[c]], vector_helps=c <= 2)
                if a == 0:
                    zts0 = turn(0, z_sbs[0])
                    zts1 = turn(1, z_sbs[1], pool=psum_z, tag="z")
                    results[0] = normalise(0, zts0)
                    results[1] = normalise(1, zts1)
                if a == 1:
                    finish(1, results[1])
                    results[2] = normalise(2, turn(2, z_sbs[2]), vector_helps=False)
        zts = [[z_banks[2 * s + j][:, 0:P] for j in range(2)] for s in range(SIDES)]
        narrow_rts = turn_back(last - 1, results[last - 1], vector_helps=False, pool=psum_z, tag="z")
        wide_rts = turn_back(last - 2, results[last - 2], vector_helps=False, pool=psum_z, tag="z")
        empty(last - 1, narrow_rts, 0, vector_helps=False)
        empty(last - 1, narrow_rts, 1, vector_helps=False)
        centred = centre(last, zts, *moments(last, zts))
        last_results = activate(last, *centred)
        empty(last - 2, wide_rts, 0, vector_helps=False)
        empty(last - 2, wide_rts, 1, vector_helps=False)
        store_what_is_ready()
        finish(last, last_results, pool=psum_z, tag="z")
        store_what_is_ready()
